import numpy as np
import ml_dtypes


def mxq(x, axis, fmt="e4m3"):
    dtype, down = {"e4m3": (ml_dtypes.float8_e4m3fn, 7), "e5m2": (ml_dtypes.float8_e5m2, 14)}[fmt]
    v = np.moveaxis(np.asarray(x, np.float32).astype(ml_dtypes.bfloat16).astype(np.float64), axis, -1)
    blocks = v.reshape(v.shape[:-1] + (-1, 32))
    amax = np.abs(blocks).max(-1, keepdims=True)
    byte = np.maximum(np.where(amax > 0, np.frexp(amax)[1] - 1 + 127, 0) - down, 1)
    scale = np.exp2(byte - 127.0)
    codes = (blocks / scale).astype(np.float32).astype(dtype).astype(np.float64)
    return np.moveaxis((codes * scale).reshape(v.shape), -1, axis)


WIDE = False


def mx_kscale(k):
    if not WIDE:
        return np.ones(k)
    levels = np.array([10, -10, 5, -5, 0])
    if k % 512:
        return np.exp2(np.random.permutation(np.resize(levels, k // 32))).repeat(32)
    a = np.empty((k // 512, 16))
    for p in range(k // 512):
        a[p, :8] = np.random.permutation(np.resize(levels, 8))
        for g in range(8):
            far = levels[np.abs(levels - a[p, g]) >= 10]
            a[p, g + 8] = far[np.random.randint(len(far))]
    return np.exp2(a.ravel()).repeat(32)


BF16 = ml_dtypes.bfloat16


def bf(x):
    return np.asarray(x, np.float32).astype(BF16)


def f64(x):
    return np.asarray(x).astype(np.float64)


B, S, H, NH, NKV, HD = 1, 512, 2048, 16, 4, 128
NT = NH + 2 * NKV
ROPE_THETA = 10000.0


def rope(t, cos, sin):
    t2 = t.reshape(t.shape[:-1] + (HD // 2, 2))
    t0, t1 = t2[..., 0], t2[..., 1]
    c = cos[None, :, None, :]
    s = sin[None, :, None, :]
    r0 = t0 * c - t1 * s
    r1 = t0 * s + t1 * c
    return np.stack([r0, r1], axis=-1).reshape(t.shape)


def draw0():
    s = mx_kscale(H)
    inv_freq = 1.0 / (ROPE_THETA ** (np.arange(0, HD, 2) / HD))
    freqs = np.outer(np.arange(S), inv_freq)
    return {"x": bf(np.random.standard_normal((B, S, H)) * s),
            "w_qkv": bf(np.random.standard_normal((H, NT * HD)) / np.sqrt(H) / s[:, None]),
            "cos": bf(np.cos(freqs)), "sin": bf(np.sin(freqs))}


def core(x, w_qkv, cos, sin):
    xqkv = (mxq(f64(x), 2, "e4m3") @ mxq(f64(w_qkv), 0, "e4m3")).reshape(B, S, NT, HD)
    xq = xqkv[:, :, :NH]
    xk = xqkv[:, :, NH:NH + NKV]
    xv = xqkv[:, :, NH + NKV:]
    return rope(xq, f64(cos), f64(sin)), rope(xk, f64(cos), f64(sin)), xv


def e4m3fn_bytes(y):
    return np.clip(np.asarray(y, np.float64), -448.0, 448.0).astype(np.float32).astype(ml_dtypes.float8_e4m3fn).view(np.uint8)


def e4m3fn_values(b):
    return np.asarray(b, np.uint8).view(ml_dtypes.float8_e4m3fn).astype(np.float64)


def setup_inputs():
    d = draw0()
    x0 = np.asarray(d['w_qkv']).astype(np.float64)
    s = (np.max(np.abs(x0), axis=(1,), keepdims=True) / 448.0).astype(np.float32)
    out = {}
    for k, v in d.items():
        if k == 'w_qkv':
            out['w_qkv_bytes'] = e4m3fn_bytes(x0 / s.astype(np.float64))
            out['w_qkv_scale'] = s
        else:
            out[k] = v
    return out


def reference(x, w_qkv_bytes, w_qkv_scale, cos, sin):
    return core(x, e4m3fn_values(w_qkv_bytes) * w_qkv_scale.astype(np.float64), cos, sin)

@@ -1,0 +1,247 @@
+from contextlib import ExitStack
+
+import concourse.mybir as mybir
+from concourse.masks import make_identity
+
+F32 = mybir.dt.float32
+BF16 = mybir.dt.bfloat16
+U32 = mybir.dt.uint32
+U8 = mybir.dt.uint8
+FP8 = mybir.dt.float8_e4m3fn
+FP8X4 = mybir.dt.float8_e4m3fn_x4
+MULT = mybir.AluOpType.mult
+ADD = mybir.AluOpType.add
+COPY = mybir.ActivationFunctionType.Copy
+
+TOKENS, HIDDEN, FEATURES = 512, 2048, 3072
+FLOPS = 2 * TOKENS * HIDDEN * FEATURES
+
+P = 128
+PACK = 4
+PASSES = HIDDEN // (P * PACK)
+TOKEN_TILES = TOKENS // P
+CHUNK = 512
+CHUNKS = FEATURES // CHUNK
+ROPE_CHUNKS = 5
+UNITS = CHUNKS * PASSES
+HEAD = 128
+SCALAR_COLS = 176
+
+
+def tile_quantllamaattentionfused_pa_kernel(tc, x, w_qkv_bytes, w_qkv_scale, cos, sin, out_0, out_1, out_2):
+    nc = tc.nc
+    x_rows = x.rearrange("b s h -> (b s) h")
+    w_view = w_qkv_bytes.rearrange("(g p t) n -> g p t n", p=P, t=PACK)
+    q_rows = out_0.rearrange("b s h d -> (b s) (h d)")
+    k_rows = out_1.rearrange("b s h d -> (b s) (h d)")
+    v_rows = out_2.rearrange("b s h d -> (b s) (h d)")
+
+    def out_block(c, m):
+        rows = slice(m * P, (m + 1) * P)
+        if c < 4:
+            return q_rows[rows, c * CHUNK : (c + 1) * CHUNK]
+        if c == 4:
+            return k_rows[rows, :]
+        return v_rows[rows, :]
+
+    with ExitStack() as ctx:
+        const = ctx.enter_context(tc.tile_pool(name="const", bufs=1))
+        xin_pool = ctx.enter_context(tc.tile_pool(name="xin", bufs=TOKEN_TILES))
+        xq_pool = ctx.enter_context(tc.tile_pool(name="xq", bufs=TOKEN_TILES))
+        wb_pool = ctx.enter_context(tc.tile_pool(name="wbytes", bufs=UNITS))
+        wide_pool = ctx.enter_context(tc.tile_pool(name="wide", bufs=4))
+        grp_pool = ctx.enter_context(tc.tile_pool(name="grp", bufs=3))
+        code_pool = ctx.enter_context(tc.tile_pool(name="codes", bufs=6))
+        rope_pool = ctx.enter_context(tc.tile_pool(name="rope", bufs=3))
+        res_pool = ctx.enter_context(tc.tile_pool(name="res", bufs=4))
+        psum = ctx.enter_context(tc.psum_pool(name="psum", bufs=8))
+        ctx.enter_context(tc.manual_schedule())
+
+        ident = const.tile([P, P], F32, name="ident")
+        make_identity(nc, ident[:])
+
+        w_scale = const.tile([P, PASSES, PACK], F32, name="w_scale")
+        nc.scalar.dma_start(out=w_scale[:], in_=w_qkv_scale.rearrange("(g p t) o -> p g (t o)", p=P, t=PACK))
+        cos_in = const.tile([P, TOKEN_TILES, HEAD // 2], BF16, name="cos_in")
+        nc.scalar.dma_start(out=cos_in[:], in_=cos.rearrange("(m p) j -> p m j", p=P))
+        sin_in = const.tile([P, TOKEN_TILES, HEAD // 2], BF16, name="sin_in")
+        nc.scalar.dma_start(out=sin_in[:], in_=sin.rearrange("(m p) j -> p m j", p=P))
+
+        w_bytes = []
+        x_in = []
+        for u in range(UNITS):
+            c, g = divmod(u, PASSES)
+            wb = wb_pool.tile([P, PACK, CHUNK], U8, name="wb", tag="wb")
+            nc.sync.dma_start(out=wb[:], in_=w_view[g][:, :, c * CHUNK : (c + 1) * CHUNK])
+            w_bytes.append(wb)
+            if u < TOKEN_TILES:
+                xi = xin_pool.tile([P, HIDDEN], BF16, name="xi", tag="xi")
+                nc.sync.dma_start(out=xi[:], in_=x_rows[u * P : (u + 1) * P, :])
+                x_in.append(xi)
+
+        cos2 = const.tile([P, TOKEN_TILES, HEAD], F32, name="cos2")
+        sin2 = const.tile([P, TOKEN_TILES, HEAD], F32, name="sin2")
+        cos2_v = cos2[:].rearrange("p m (j e) -> p m j e", e=2)
+        sin2_v = sin2[:].rearrange("p m (j e) -> p m j e", e=2)
+        nc.vector.tensor_copy(out=cos2_v[:, :, :, 0], in_=cos_in[:])
+        nc.vector.tensor_copy(out=cos2_v[:, :, :, 1], in_=cos_in[:])
+        nc.vector.tensor_copy(out=sin2_v[:, :, :, 0], in_=sin_in[:])
+        nc.vector.tensor_scalar(out=sin2_v[:, :, :, 1], in0=sin_in[:], scalar1=-1.0, scalar2=None, op0=MULT)
+
+        wide = {}
+        grouped = {}
+        w_codes = {}
+        x_banks = {}
+        x_grouped = {}
+        x_codes = {}
+        acc = {}
+        prod = {}
+
+        def widen(u):
+            g = u % PASSES
+            wd = wide_pool.tile([P, PACK, CHUNK], BF16, name="wd", tag="wd")
+            for t in range(PACK):
+                nc.scalar.activation(
+                    out=wd[:, t, :], in_=w_bytes[u][:, t, :].bitcast(FP8), func=COPY, scale=w_scale[:, g, t : t + 1]
+                )
+            wide[u] = wd
+
+        def interleave(u, scalar_cols):
+            gr = grp_pool.tile([P, CHUNK, PACK], BF16, name="gr", tag="gr", align_bytes=64)
+            cut = CHUNK - scalar_cols
+            wd = wide[u]
+            if cut > 0:
+                nc.vector.tensor_copy(out=gr[:, :cut, :], in_=wd[:, :, :cut].rearrange("p t n -> p n t"))
+            if scalar_cols > 0:
+                nc.scalar.copy(out=gr[:, cut:, :], in_=wd[:, :, cut:].rearrange("p t n -> p n t"))
+            grouped[u] = gr
+
+        def quantize_w(u):
+            wc = code_pool.tile([P, CHUNK], U32, name="wc", tag="wc", align_bytes=64)
+            ws = code_pool.tile([P, CHUNK], U8, name="ws", tag="ws", align_bytes=64)
+            nc.vector.quantize_mx(
+                out=wc[:].bitcast(FP8X4), scales=ws[:], in_=grouped[u][:].rearrange("p n t -> p (n t)")
+            )
+            w_codes[u] = (wc, ws)
+
+        def x_transposes(m):
+            words = x_in[m][:].bitcast(F32)
+            banks = []
+            for half in range(2):
+                xt = psum.tile([P, CHUNK], F32, name="acc", tag="acc")
+                for q in range(4):
+                    g = 2 * half + q // 2
+                    first = 256 * g + q % 2
+                    nc.tensor.transpose(xt[:, q * P : (q + 1) * P], words[:, first : 256 * (g + 1) : 2], ident[:])
+                banks.append(xt)
+            x_banks[m] = banks
+
+        def x_copies(m):
+            xg = xq_pool.tile([P, PASSES * P * PACK], BF16, name="xg", tag="xg", align_bytes=64)
+            xg_words = xg[:].bitcast(F32).rearrange("p (g r u) -> p g r u", g=PASSES, u=2)
+            for half in range(2):
+                nc.vector.tensor_copy(
+                    out=xg_words[:, 2 * half : 2 * half + 2],
+                    in_=x_banks[m][half][:].rearrange("p (g u r) -> p g r u", g=2, u=2),
+                )
+            x_grouped[m] = xg
+
+        def quantize_x(m):
+            xc = xq_pool.tile([P, PASSES * P], U32, name="xc", tag="xc", align_bytes=64)
+            xs = xq_pool.tile([P, PASSES * P], U8, name="xs", tag="xs", align_bytes=64)
+            nc.vector.quantize_mx(out=xc[:].bitcast(FP8X4), scales=xs[:], in_=x_grouped[m][:])
+            x_codes[m] = (xc, xs)
+
+        def multiply(u, m):
+            c, g = divmod(u, PASSES)
+            if g == 0:
+                bank = psum.tile([P, CHUNK], F32, name="acc", tag="acc")
+                acc[(c, m)] = bank
+            xc, xs = x_codes[m]
+            wc, ws = w_codes[u]
+            cols = slice(g * P, (g + 1) * P)
+            nc.tensor.matmul_mx(
+                out=acc[(c, m)][:],
+                lhsT=xc[:, cols].bitcast(FP8X4),
+                lhsT_scale=xs[:, cols],
+                rhs=wc[:].bitcast(FP8X4),
+                rhs_scale=ws[:],
+                start=(g == 0),
+                stop=(g == PASSES - 1),
+            )
+
+        def rope_products(c, m):
+            pa = rope_pool.tile([P, CHUNK], F32, name="pa", tag="pa")
+            pb = rope_pool.tile([P, CHUNK], F32, name="pb", tag="pb")
+            heads = acc[(c, m)][:].rearrange("p (h f) -> p h f", f=HEAD)
+            shape = [P, CHUNK // HEAD, HEAD]
+            nc.vector.tensor_tensor(
+                out=pa[:].rearrange("p (h f) -> p h f", f=HEAD),
+                in0=heads,
+                in1=cos2[:, m, :].unsqueeze(1).to_broadcast(shape),
+                op=MULT,
+            )
+            nc.vector.tensor_tensor(
+                out=pb[:].rearrange("p (h f) -> p h f", f=HEAD),
+                in0=heads,
+                in1=sin2[:, m, :].unsqueeze(1).to_broadcast(shape),
+                op=MULT,
+            )
+            prod[(c, m)] = (pa, pb)
+
+        def rope_sum(c, m):
+            pa, pb = prod[(c, m)]
+            res = res_pool.tile([P, CHUNK], F32, name="res", tag="res")
+            nc.vector.tensor_tensor(
+                out=res[:].rearrange("p (j e) -> p j e", e=2),
+                in0=pa[:].rearrange("p (j e) -> p j e", e=2),
+                in1=pb[:].rearrange("p (j e) -> p j e", e=2)[:, :, ::-1],
+                op=ADD,
+            )
+            nc.sync.dma_start(out=out_block(c, m), in_=res[:])
+
+        def plain_copy(c, m, on_scalar):
+            res = res_pool.tile([P, CHUNK], F32, name="res", tag="res")
+            if on_scalar:
+                nc.scalar.copy(out=res[:], in_=acc[(c, m)][:])
+            else:
+                nc.vector.tensor_copy(out=res[:], in_=acc[(c, m)][:])
+            nc.sync.dma_start(out=out_block(c, m), in_=res[:])
+
+        for m in range(TOKEN_TILES):
+            x_transposes(m)
+        widen(0)
+        widen(1)
+        x_copies(0)
+        interleave(0, SCALAR_COLS)
+
+        for tick in range(UNITS - 1):
+            if tick + 2 < UNITS:
+                widen(tick + 2)
+            interleave(tick + 1, {UNITS - 1: CHUNK, UNITS - 2: 256}.get(tick + 1, SCALAR_COLS))
+            piece = tick - PASSES
+            if tick + 1 < TOKEN_TILES:
+                x_copies(tick + 1)
+            if piece >= 0:
+                rope_products(piece // TOKEN_TILES, piece % TOKEN_TILES)
+            quantize_w(tick)
+            if tick < TOKEN_TILES:
+                quantize_x(tick)
+            if piece >= 0:
+                rope_sum(piece // TOKEN_TILES, piece % TOKEN_TILES)
+            if tick == PASSES - 1:
+                for m in range(TOKEN_TILES):
+                    for g in range(PASSES):
+                        multiply(g, m)
+            if tick >= PASSES:
+                for m in range(TOKEN_TILES):
+                    multiply(tick, m)
+
+        quantize_w(UNITS - 1)
+        for m in range(TOKEN_TILES):
+            multiply(UNITS - 1, m)
+        rope_products(ROPE_CHUNKS - 1, TOKEN_TILES - 1)
+        for m in range(TOKEN_TILES - 1):
+            plain_copy(CHUNKS - 1, m, True)
+        rope_sum(ROPE_CHUNKS - 1, TOKEN_TILES - 1)
+        plain_copy(CHUNKS - 1, TOKEN_TILES - 1, True)

@@ -25,7 +25,8 @@ CHUNKS = FEATURES // CHUNK
 ROPE_CHUNKS = 5
 UNITS = CHUNKS * PASSES
 HEAD = 128
-SCALAR_COLS = 176
+SCALAR_COLS = 48
+TENSOR_COLS = 192
 
 
 def tile_quantllamaattentionfused_pa_kernel(tc, x, w_qkv_bytes, w_qkv_scale, cos, sin, out_0, out_1, out_2):
@@ -54,11 +55,14 @@ def tile_quantllamaattentionfused_pa_kernel(tc, x, w_qkv_bytes, w_qkv_scale, cos
         code_pool = ctx.enter_context(tc.tile_pool(name="codes", bufs=6))
         rope_pool = ctx.enter_context(tc.tile_pool(name="rope", bufs=3))
         res_pool = ctx.enter_context(tc.tile_pool(name="res", bufs=4))
-        psum = ctx.enter_context(tc.psum_pool(name="psum", bufs=8))
+        psum = ctx.enter_context(tc.psum_pool(name="psum", bufs=6))
+        psum_il = ctx.enter_context(tc.psum_pool(name="psum_il", bufs=2))
         ctx.enter_context(tc.manual_schedule())
 
         ident = const.tile([P, P], F32, name="ident")
         make_identity(nc, ident[:])
+        ident_bf = const.tile([P, P], BF16, name="ident_bf")
+        make_identity(nc, ident_bf[:])
 
         w_scale = const.tile([P, PASSES, PACK], F32, name="w_scale")
         nc.scalar.dma_start(out=w_scale[:], in_=w_qkv_scale.rearrange("(g p t) o -> p g (t o)", p=P, t=PACK))
@@ -89,6 +93,7 @@ def tile_quantllamaattentionfused_pa_kernel(tc, x, w_qkv_bytes, w_qkv_scale, cos
         nc.vector.tensor_scalar(out=sin2_v[:, :, :, 1], in0=sin_in[:], scalar1=-1.0, scalar2=None, op0=MULT)
 
         wide = {}
+        passed = {}
         grouped = {}
         w_codes = {}
         x_banks = {}
@@ -106,12 +111,30 @@ def tile_quantllamaattentionfused_pa_kernel(tc, x, w_qkv_bytes, w_qkv_scale, cos
                 )
             wide[u] = wd
 
+        def pass_through(u):
+            pil = psum_il.tile([P, 2 * CHUNK], BF16, name="pil", tag="pil")
+            wd = wide[u]
+            for n0, n1 in ((0, 128), (128, TENSOR_COLS)):
+                nc.tensor.matmul(
+                    out=pil[:, n0 * PACK : n1 * PACK].rearrange("p (n t) -> p n t", t=PACK),
+                    lhsT=ident_bf[:],
+                    rhs=wd[:, :, n0:n1].rearrange("p t n -> p n t"),
+                    start=True,
+                    stop=True,
+                )
+            passed[u] = pil
+
         def interleave(u, scalar_cols):
             gr = grp_pool.tile([P, CHUNK, PACK], BF16, name="gr", tag="gr", align_bytes=64)
             cut = CHUNK - scalar_cols
             wd = wide[u]
-            if cut > 0:
-                nc.vector.tensor_copy(out=gr[:, :cut, :], in_=wd[:, :, :cut].rearrange("p t n -> p n t"))
+            nc.scalar.copy(
+                out=gr[:, :TENSOR_COLS, :].rearrange("p n t -> p (n t)"), in_=passed[u][:, : TENSOR_COLS * PACK]
+            )
+            if cut > TENSOR_COLS:
+                nc.vector.tensor_copy(
+                    out=gr[:, TENSOR_COLS:cut, :], in_=wd[:, :, TENSOR_COLS:cut].rearrange("p t n -> p n t")
+                )
             if scalar_cols > 0:
                 nc.scalar.copy(out=gr[:, cut:, :], in_=wd[:, :, cut:].rearrange("p t n -> p n t"))
             grouped[u] = gr
@@ -208,17 +231,21 @@ def tile_quantllamaattentionfused_pa_kernel(tc, x, w_qkv_bytes, w_qkv_scale, cos
                 nc.vector.tensor_copy(out=res[:], in_=acc[(c, m)][:])
             nc.sync.dma_start(out=out_block(c, m), in_=res[:])
 
-        for m in range(TOKEN_TILES):
-            x_transposes(m)
+        x_transposes(0)
         widen(0)
+        pass_through(0)
         widen(1)
+        pass_through(1)
         x_copies(0)
         interleave(0, SCALAR_COLS)
 
         for tick in range(UNITS - 1):
             if tick + 2 < UNITS:
                 widen(tick + 2)
-            interleave(tick + 1, {UNITS - 1: CHUNK, UNITS - 2: 256}.get(tick + 1, SCALAR_COLS))
+                pass_through(tick + 2)
+            if tick + 1 < TOKEN_TILES:
+                x_transposes(tick + 1)
+            interleave(tick + 1, {UNITS - 1: CHUNK - TENSOR_COLS, UNITS - 2: 160}.get(tick + 1, SCALAR_COLS))
             piece = tick - PASSES
             if tick + 1 < TOKEN_TILES:
                 x_copies(tick + 1)
@@ -234,7 +261,9 @@ def tile_quantllamaattentionfused_pa_kernel(tc, x, w_qkv_bytes, w_qkv_scale, cos
                     for g in range(PASSES):
                         multiply(g, m)
             if tick >= PASSES:
-                for m in range(TOKEN_TILES):
+                if tick % PASSES == 1:
+                    multiply(tick - 1, TOKEN_TILES - 1)
+                for m in range(TOKEN_TILES - 1 if tick % PASSES == 0 else TOKEN_TILES):
                     multiply(tick, m)
 
         quantize_w(UNITS - 1)

@@ -25,7 +25,7 @@ CHUNKS = FEATURES // CHUNK
 ROPE_CHUNKS = 5
 UNITS = CHUNKS * PASSES
 HEAD = 128
-SCALAR_COLS = 48
+SCALAR_COLS = 64
 TENSOR_COLS = 192
 
 
@@ -50,11 +50,11 @@ def tile_quantllamaattentionfused_pa_kernel(tc, x, w_qkv_bytes, w_qkv_scale, cos
         xin_pool = ctx.enter_context(tc.tile_pool(name="xin", bufs=TOKEN_TILES))
         xq_pool = ctx.enter_context(tc.tile_pool(name="xq", bufs=TOKEN_TILES))
         wb_pool = ctx.enter_context(tc.tile_pool(name="wbytes", bufs=UNITS))
-        wide_pool = ctx.enter_context(tc.tile_pool(name="wide", bufs=4))
-        grp_pool = ctx.enter_context(tc.tile_pool(name="grp", bufs=3))
-        code_pool = ctx.enter_context(tc.tile_pool(name="codes", bufs=6))
-        rope_pool = ctx.enter_context(tc.tile_pool(name="rope", bufs=3))
-        res_pool = ctx.enter_context(tc.tile_pool(name="res", bufs=4))
+        wide_pool = ctx.enter_context(tc.tile_pool(name="wide", bufs=6))
+        grp_pool = ctx.enter_context(tc.tile_pool(name="grp", bufs=5))
+        code_pool = ctx.enter_context(tc.tile_pool(name="codes", bufs=8))
+        rope_pool = ctx.enter_context(tc.tile_pool(name="rope", bufs=5))
+        res_pool = ctx.enter_context(tc.tile_pool(name="res", bufs=8))
         psum = ctx.enter_context(tc.psum_pool(name="psum", bufs=6))
         psum_il = ctx.enter_context(tc.psum_pool(name="psum_il", bufs=2))
         ctx.enter_context(tc.manual_schedule())
@@ -231,21 +231,25 @@ def tile_quantllamaattentionfused_pa_kernel(tc, x, w_qkv_bytes, w_qkv_scale, cos
                 nc.vector.tensor_copy(out=res[:], in_=acc[(c, m)][:])
             nc.sync.dma_start(out=out_block(c, m), in_=res[:])
 
-        x_transposes(0)
-        widen(0)
-        pass_through(0)
-        widen(1)
-        pass_through(1)
+        def scalar_cols(u):
+            if u < PASSES:
+                return 0
+            return {UNITS - 1: CHUNK - TENSOR_COLS, UNITS - 2: 160}.get(u, SCALAR_COLS)
+
+        for u in range(2):
+            x_transposes(u)
+            widen(u)
+            pass_through(u)
         x_copies(0)
-        interleave(0, SCALAR_COLS)
+        interleave(0, scalar_cols(0))
 
         for tick in range(UNITS - 1):
+            if tick + 2 < TOKEN_TILES:
+                x_transposes(tick + 2)
             if tick + 2 < UNITS:
                 widen(tick + 2)
                 pass_through(tick + 2)
-            if tick + 1 < TOKEN_TILES:
-                x_transposes(tick + 1)
-            interleave(tick + 1, {UNITS - 1: CHUNK - TENSOR_COLS, UNITS - 2: 160}.get(tick + 1, SCALAR_COLS))
+            interleave(tick + 1, scalar_cols(tick + 1))
             piece = tick - PASSES
             if tick + 1 < TOKEN_TILES:
                 x_copies(tick + 1)
@@ -271,6 +275,6 @@ def tile_quantllamaattentionfused_pa_kernel(tc, x, w_qkv_bytes, w_qkv_scale, cos
             multiply(UNITS - 1, m)
         rope_products(ROPE_CHUNKS - 1, TOKEN_TILES - 1)
         for m in range(TOKEN_TILES - 1):
-            plain_copy(CHUNKS - 1, m, True)
+            plain_copy(CHUNKS - 1, m, m != 1)
         rope_sum(ROPE_CHUNKS - 1, TOKEN_TILES - 1)
         plain_copy(CHUNKS - 1, TOKEN_TILES - 1, True)

@@ -27,6 +27,7 @@ UNITS = CHUNKS * PASSES
 HEAD = 128
 SCALAR_COLS = 64
 TENSOR_COLS = 192
+GPSIMD_COLS = 128
 
 
 def tile_quantllamaattentionfused_pa_kernel(tc, x, w_qkv_bytes, w_qkv_scale, cos, sin, out_0, out_1, out_2):
@@ -51,7 +52,7 @@ def tile_quantllamaattentionfused_pa_kernel(tc, x, w_qkv_bytes, w_qkv_scale, cos
         xq_pool = ctx.enter_context(tc.tile_pool(name="xq", bufs=TOKEN_TILES))
         wb_pool = ctx.enter_context(tc.tile_pool(name="wbytes", bufs=UNITS))
         wide_pool = ctx.enter_context(tc.tile_pool(name="wide", bufs=6))
-        grp_pool = ctx.enter_context(tc.tile_pool(name="grp", bufs=5))
+        grp_pool = ctx.enter_context(tc.tile_pool(name="grp", bufs=2))
         code_pool = ctx.enter_context(tc.tile_pool(name="codes", bufs=8))
         rope_pool = ctx.enter_context(tc.tile_pool(name="rope", bufs=5))
         res_pool = ctx.enter_context(tc.tile_pool(name="res", bufs=8))
@@ -124,20 +125,45 @@ def tile_quantllamaattentionfused_pa_kernel(tc, x, w_qkv_bytes, w_qkv_scale, cos
                 )
             passed[u] = pil
 
-        def interleave(u, scalar_cols):
-            gr = grp_pool.tile([P, CHUNK, PACK], BF16, name="gr", tag="gr", align_bytes=64)
-            cut = CHUNK - scalar_cols
-            wd = wide[u]
+        def group(u):
+            if u not in grouped:
+                gr = grp_pool.tile([P, CHUNK, PACK], BF16, name="gr", tag="gr", align_bytes=64)
+                grouped[u] = gr
+            return grouped[u]
+
+        def bounds(u):
+            s_cols = scalar_cols(u)
+            v_end = CHUNK - s_cols - GPSIMD_COLS
+            return v_end, CHUNK - s_cols
+
+        def interleave_g(u):
+            gr = group(u)
+            a, b = bounds(u)
+            nc.gpsimd.tensor_scalar(
+                out=gr[:, a:b, :],
+                in0=wide[u][:, :, a:b].rearrange("p t n -> p n t"),
+                scalar1=1.0,
+                scalar2=0.0,
+                op0=MULT,
+                op1=ADD,
+            )
+
+        def interleave_s(u):
+            gr = group(u)
+            cut = bounds(u)[1]
             nc.scalar.copy(
                 out=gr[:, :TENSOR_COLS, :].rearrange("p n t -> p (n t)"), in_=passed[u][:, : TENSOR_COLS * PACK]
             )
-            if cut > TENSOR_COLS:
+            if cut < CHUNK:
+                nc.scalar.copy(out=gr[:, cut:, :], in_=wide[u][:, :, cut:].rearrange("p t n -> p n t"))
+
+        def interleave_v(u):
+            gr = group(u)
+            v_end = bounds(u)[0]
+            if v_end > TENSOR_COLS:
                 nc.vector.tensor_copy(
-                    out=gr[:, TENSOR_COLS:cut, :], in_=wd[:, :, TENSOR_COLS:cut].rearrange("p t n -> p n t")
+                    out=gr[:, TENSOR_COLS:v_end, :], in_=wide[u][:, :, TENSOR_COLS:v_end].rearrange("p t n -> p n t")
                 )
-            if scalar_cols > 0:
-                nc.scalar.copy(out=gr[:, cut:, :], in_=wd[:, :, cut:].rearrange("p t n -> p n t"))
-            grouped[u] = gr
 
         def quantize_w(u):
             wc = code_pool.tile([P, CHUNK], U32, name="wc", tag="wc", align_bytes=64)
@@ -234,47 +260,63 @@ def tile_quantllamaattentionfused_pa_kernel(tc, x, w_qkv_bytes, w_qkv_scale, cos
         def scalar_cols(u):
             if u < PASSES:
                 return 0
-            return {UNITS - 1: CHUNK - TENSOR_COLS, UNITS - 2: 160}.get(u, SCALAR_COLS)
+            return {UNITS - 1: 192, UNITS - 2: 192, UNITS - 3: 128}.get(u, SCALAR_COLS)
 
-        for u in range(2):
-            x_transposes(u)
-            widen(u)
-            pass_through(u)
+        x_transposes(0)
+        x_transposes(1)
+        widen(0)
+        pass_through(0)
+        widen(1)
+        pass_through(1)
+        interleave_g(0)
+        interleave_s(0)
         x_copies(0)
-        interleave(0, scalar_cols(0))
+        interleave_v(0)
+        x_transposes(2)
+        widen(2)
+        pass_through(2)
+        interleave_g(1)
+        interleave_s(1)
+        quantize_x(0)
+        x_copies(1)
+        interleave_v(1)
 
-        for tick in range(UNITS - 1):
-            if tick + 2 < TOKEN_TILES:
-                x_transposes(tick + 2)
-            if tick + 2 < UNITS:
-                widen(tick + 2)
-                pass_through(tick + 2)
-            interleave(tick + 1, scalar_cols(tick + 1))
+        for tick in range(UNITS):
             piece = tick - PASSES
-            if tick + 1 < TOKEN_TILES:
-                x_copies(tick + 1)
+            last = tick == UNITS - 1
+            if tick == 0:
+                x_transposes(3)
+            if tick + 3 < UNITS:
+                widen(tick + 3)
+            quantize_w(tick)
+            if tick + 2 < UNITS:
+                interleave_g(tick + 2)
+            if tick + 2 < TOKEN_TILES:
+                x_copies(tick + 2)
+            if last:
+                for m in range(TOKEN_TILES):
+                    multiply(tick, m)
             if piece >= 0:
                 rope_products(piece // TOKEN_TILES, piece % TOKEN_TILES)
-            quantize_w(tick)
-            if tick < TOKEN_TILES:
-                quantize_x(tick)
-            if piece >= 0:
-                rope_sum(piece // TOKEN_TILES, piece % TOKEN_TILES)
             if tick == PASSES - 1:
                 for m in range(TOKEN_TILES):
                     for g in range(PASSES):
                         multiply(g, m)
-            if tick >= PASSES:
+            if tick >= PASSES and not last:
                 if tick % PASSES == 1:
                     multiply(tick - 1, TOKEN_TILES - 1)
                 for m in range(TOKEN_TILES - 1 if tick % PASSES == 0 else TOKEN_TILES):
                     multiply(tick, m)
-
-        quantize_w(UNITS - 1)
-        for m in range(TOKEN_TILES):
-            multiply(UNITS - 1, m)
-        rope_products(ROPE_CHUNKS - 1, TOKEN_TILES - 1)
-        for m in range(TOKEN_TILES - 1):
-            plain_copy(CHUNKS - 1, m, m != 1)
-        rope_sum(ROPE_CHUNKS - 1, TOKEN_TILES - 1)
+            if tick + 3 < UNITS:
+                pass_through(tick + 3)
+            if tick + 2 < UNITS:
+                interleave_s(tick + 2)
+                interleave_v(tick + 2)
+            if tick + 1 < TOKEN_TILES:
+                quantize_x(tick + 1)
+            if last:
+                for m in range(TOKEN_TILES - 1):
+                    plain_copy(CHUNKS - 1, m, m != 1)
+            if piece >= 0:
+                rope_sum(piece // TOKEN_TILES, piece % TOKEN_TILES)
         plain_copy(CHUNKS - 1, TOKEN_TILES - 1, True)

@@ -25,9 +25,9 @@ CHUNKS = FEATURES // CHUNK
 ROPE_CHUNKS = 5
 UNITS = CHUNKS * PASSES
 HEAD = 128
-SCALAR_COLS = 64
+SCALAR_COLS = 0
 TENSOR_COLS = 192
-GPSIMD_COLS = 128
+GPSIMD_COLS = 160
 
 
 def tile_quantllamaattentionfused_pa_kernel(tc, x, w_qkv_bytes, w_qkv_scale, cos, sin, out_0, out_1, out_2):
@@ -260,7 +260,7 @@ def tile_quantllamaattentionfused_pa_kernel(tc, x, w_qkv_bytes, w_qkv_scale, cos
         def scalar_cols(u):
             if u < PASSES:
                 return 0
-            return {UNITS - 1: 192, UNITS - 2: 192, UNITS - 3: 128}.get(u, SCALAR_COLS)
+            return {UNITS - 1: 160, UNITS - 2: 160, UNITS - 3: 96}.get(u, SCALAR_COLS)
 
         x_transposes(0)
         x_transposes(1)

@@ -84,10 +84,9 @@ def tile_quantllamaattentionfused_pa_kernel(tc, x, w_qkv_bytes, w_qkv_scale, cos
                 nc.sync.dma_start(out=xi[:], in_=x_rows[u * P : (u + 1) * P, :])
                 x_in.append(xi)
 
-        cos2 = const.tile([P, TOKEN_TILES, HEAD], F32, name="cos2")
-        sin2 = const.tile([P, TOKEN_TILES, HEAD], F32, name="sin2")
-        cos2_v = cos2[:].rearrange("p m (j e) -> p m j e", e=2)
-        sin2_v = sin2[:].rearrange("p m (j e) -> p m j e", e=2)
+        tables = const.tile([P, TOKEN_TILES, 2, HEAD], F32, name="tables")
+        cos2_v = tables[:, :, 0, :].rearrange("p m (j e) -> p m j e", e=2)
+        sin2_v = tables[:, :, 1, :].rearrange("p m (j e) -> p m j e", e=2)
         nc.vector.tensor_copy(out=cos2_v[:, :, :, 0], in_=cos_in[:])
         nc.vector.tensor_copy(out=cos2_v[:, :, :, 1], in_=cos_in[:])
         nc.vector.tensor_copy(out=sin2_v[:, :, :, 0], in_=sin_in[:])
@@ -220,31 +219,23 @@ def tile_quantllamaattentionfused_pa_kernel(tc, x, w_qkv_bytes, w_qkv_scale, cos
             )
 
         def rope_products(c, m):
-            pa = rope_pool.tile([P, CHUNK], F32, name="pa", tag="pa")
-            pb = rope_pool.tile([P, CHUNK], F32, name="pb", tag="pb")
-            heads = acc[(c, m)][:].rearrange("p (h f) -> p h f", f=HEAD)
-            shape = [P, CHUNK // HEAD, HEAD]
+            pab = rope_pool.tile([P, 2, CHUNK], F32, name="pab", tag="pab")
+            shape = [P, 2, CHUNK // HEAD, HEAD]
             nc.vector.tensor_tensor(
-                out=pa[:].rearrange("p (h f) -> p h f", f=HEAD),
-                in0=heads,
-                in1=cos2[:, m, :].unsqueeze(1).to_broadcast(shape),
+                out=pab[:].rearrange("p s (h f) -> p s h f", f=HEAD),
+                in0=acc[(c, m)][:].rearrange("p (h f) -> p h f", f=HEAD).unsqueeze(1).to_broadcast(shape),
+                in1=tables[:, m, :, :].unsqueeze(2).to_broadcast(shape),
                 op=MULT,
             )
-            nc.vector.tensor_tensor(
-                out=pb[:].rearrange("p (h f) -> p h f", f=HEAD),
-                in0=heads,
-                in1=sin2[:, m, :].unsqueeze(1).to_broadcast(shape),
-                op=MULT,
-            )
-            prod[(c, m)] = (pa, pb)
+            prod[(c, m)] = pab
 
         def rope_sum(c, m):
-            pa, pb = prod[(c, m)]
+            pab = prod[(c, m)]
             res = res_pool.tile([P, CHUNK], F32, name="res", tag="res")
             nc.vector.tensor_tensor(
                 out=res[:].rearrange("p (j e) -> p j e", e=2),
-                in0=pa[:].rearrange("p (j e) -> p j e", e=2),
-                in1=pb[:].rearrange("p (j e) -> p j e", e=2)[:, :, ::-1],
+                in0=pab[:, 0, :].rearrange("p (j e) -> p j e", e=2),
+                in1=pab[:, 1, :].rearrange("p (j e) -> p j e", e=2)[:, :, ::-1],
                 op=ADD,
             )
             nc.sync.dma_start(out=out_block(c, m), in_=res[:])
@@ -281,6 +272,9 @@ def tile_quantllamaattentionfused_pa_kernel(tc, x, w_qkv_bytes, w_qkv_scale, cos
         x_copies(1)
         interleave_v(1)
 
+        def piece_of(i):
+            return i // TOKEN_TILES, i % TOKEN_TILES
+
         for tick in range(UNITS):
             piece = tick - PASSES
             last = tick == UNITS - 1
@@ -291,13 +285,17 @@ def tile_quantllamaattentionfused_pa_kernel(tc, x, w_qkv_bytes, w_qkv_scale, cos
             quantize_w(tick)
             if tick + 2 < UNITS:
                 interleave_g(tick + 2)
+            if piece < 0:
+                interleave_v(tick + 2)
+            if piece >= 1:
+                rope_sum(*piece_of(piece - 1))
             if tick + 2 < TOKEN_TILES:
                 x_copies(tick + 2)
             if last:
                 for m in range(TOKEN_TILES):
                     multiply(tick, m)
             if piece >= 0:
-                rope_products(piece // TOKEN_TILES, piece % TOKEN_TILES)
+                rope_products(*piece_of(piece))
             if tick == PASSES - 1:
                 for m in range(TOKEN_TILES):
                     for g in range(PASSES):
@@ -311,12 +309,11 @@ def tile_quantllamaattentionfused_pa_kernel(tc, x, w_qkv_bytes, w_qkv_scale, cos
                 pass_through(tick + 3)
             if tick + 2 < UNITS:
                 interleave_s(tick + 2)
-                interleave_v(tick + 2)
+                if piece >= 0:
+                    interleave_v(tick + 2)
             if tick + 1 < TOKEN_TILES:
                 quantize_x(tick + 1)
-            if last:
-                for m in range(TOKEN_TILES - 1):
-                    plain_copy(CHUNKS - 1, m, m != 1)
-            if piece >= 0:
-                rope_sum(piece // TOKEN_TILES, piece % TOKEN_TILES)
+        for m in range(TOKEN_TILES - 1):
+            plain_copy(CHUNKS - 1, m, m != 1)
+        rope_sum(ROPE_CHUNKS - 1, TOKEN_TILES - 1)
         plain_copy(CHUNKS - 1, TOKEN_TILES - 1, True)

@@ -77,7 +77,11 @@ def tile_quantllamaattentionfused_pa_kernel(tc, x, w_qkv_bytes, w_qkv_scale, cos
         for u in range(UNITS):
             c, g = divmod(u, PASSES)
             wb = wb_pool.tile([P, PACK, CHUNK], U8, name="wb", tag="wb")
-            nc.sync.dma_start(out=wb[:], in_=w_view[g][:, :, c * CHUNK : (c + 1) * CHUNK])
+            if u == 0:
+                for t in range(PACK):
+                    nc.sync.dma_start(out=wb[:, t, :], in_=w_view[g][:, t, :CHUNK])
+            else:
+                nc.sync.dma_start(out=wb[:], in_=w_view[g][:, :, c * CHUNK : (c + 1) * CHUNK])
             w_bytes.append(wb)
             if u < TOKEN_TILES:
                 xi = xin_pool.tile([P, HIDDEN], BF16, name="xi", tag="xi")
@@ -249,9 +253,12 @@ def tile_quantllamaattentionfused_pa_kernel(tc, x, w_qkv_bytes, w_qkv_scale, cos
             nc.sync.dma_start(out=out_block(c, m), in_=res[:])
 
         def scalar_cols(u):
-            if u < PASSES:
-                return 0
-            return {UNITS - 1: 160, UNITS - 2: 160, UNITS - 3: 96}.get(u, SCALAR_COLS)
+            return 0
+
+        def piece_of(i):
+            return i // TOKEN_TILES, i % TOKEN_TILES
+
+        PIECES = ROPE_CHUNKS * TOKEN_TILES
 
         x_transposes(0)
         x_transposes(1)
@@ -272,48 +279,50 @@ def tile_quantllamaattentionfused_pa_kernel(tc, x, w_qkv_bytes, w_qkv_scale, cos
         x_copies(1)
         interleave_v(1)
 
-        def piece_of(i):
-            return i // TOKEN_TILES, i % TOKEN_TILES
-
-        for tick in range(UNITS):
-            piece = tick - PASSES
-            last = tick == UNITS - 1
+        for tick in range(UNITS - 1):
+            piece = tick - (PASSES - 1)
             if tick == 0:
                 x_transposes(3)
             if tick + 3 < UNITS:
                 widen(tick + 3)
             quantize_w(tick)
+            if tick == UNITS - 2:
+                quantize_w(tick + 1)
             if tick + 2 < UNITS:
                 interleave_g(tick + 2)
+            if tick > PASSES - 2:
+                multiply(tick, 0)
+            if tick == UNITS - 2:
+                for m in range(1, TOKEN_TILES):
+                    multiply(tick, m)
+                for m in range(TOKEN_TILES):
+                    multiply(tick + 1, m)
             if piece < 0:
                 interleave_v(tick + 2)
-            if piece >= 1:
+            if 1 <= piece <= PIECES:
                 rope_sum(*piece_of(piece - 1))
             if tick + 2 < TOKEN_TILES:
                 x_copies(tick + 2)
-            if last:
-                for m in range(TOKEN_TILES):
-                    multiply(tick, m)
-            if piece >= 0:
+            early_copy = piece >= 0 and piece % TOKEN_TILES == 0 and tick + 2 < UNITS
+            if early_copy:
+                interleave_v(tick + 2)
+            if 0 <= piece < PIECES:
                 rope_products(*piece_of(piece))
-            if tick == PASSES - 1:
-                for m in range(TOKEN_TILES):
-                    for g in range(PASSES):
+            if tick + 1 < TOKEN_TILES:
+                quantize_x(tick + 1)
+            if tick == PASSES - 2:
+                for g in range(PASSES - 1):
+                    for m in range(TOKEN_TILES):
                         multiply(g, m)
-            if tick >= PASSES and not last:
-                if tick % PASSES == 1:
-                    multiply(tick - 1, TOKEN_TILES - 1)
-                for m in range(TOKEN_TILES - 1 if tick % PASSES == 0 else TOKEN_TILES):
+            if tick > PASSES - 2 and tick < UNITS - 2:
+                for m in range(1, TOKEN_TILES):
                     multiply(tick, m)
             if tick + 3 < UNITS:
                 pass_through(tick + 3)
             if tick + 2 < UNITS:
                 interleave_s(tick + 2)
-                if piece >= 0:
+                if piece >= 0 and not early_copy:
                     interleave_v(tick + 2)
-            if tick + 1 < TOKEN_TILES:
-                quantize_x(tick + 1)
-        for m in range(TOKEN_TILES - 1):
-            plain_copy(CHUNKS - 1, m, m != 1)
+        for m in range(TOKEN_TILES):
+            plain_copy(CHUNKS - 1, m, True)
         rope_sum(ROPE_CHUNKS - 1, TOKEN_TILES - 1)
-        plain_copy(CHUNKS - 1, TOKEN_TILES - 1, True)

@@ -27,7 +27,8 @@ UNITS = CHUNKS * PASSES
 HEAD = 128
 SCALAR_COLS = 0
 TENSOR_COLS = 192
-GPSIMD_COLS = 160
+GPSIMD_COLS = 224
+LAST_GPSIMD_COLS = 128
 
 
 def tile_quantllamaattentionfused_pa_kernel(tc, x, w_qkv_bytes, w_qkv_scale, cos, sin, out_0, out_1, out_2):
@@ -136,7 +137,7 @@ def tile_quantllamaattentionfused_pa_kernel(tc, x, w_qkv_bytes, w_qkv_scale, cos
 
         def bounds(u):
             s_cols = scalar_cols(u)
-            v_end = CHUNK - s_cols - GPSIMD_COLS
+            v_end = CHUNK - s_cols - (LAST_GPSIMD_COLS if u == UNITS - 1 else GPSIMD_COLS)
             return v_end, CHUNK - s_cols
 
         def interleave_g(u):

@@ -25,10 +25,11 @@ CHUNKS = FEATURES // CHUNK
 ROPE_CHUNKS = 5
 UNITS = CHUNKS * PASSES
 HEAD = 128
-SCALAR_COLS = 0
 TENSOR_COLS = 192
-GPSIMD_COLS = 224
+GPSIMD_COLS = 192
 LAST_GPSIMD_COLS = 128
+HEAD_GPSIMD_COLS = 0
+VECTOR_PLANES = (2, 2, 2, 2)
 
 
 def tile_quantllamaattentionfused_pa_kernel(tc, x, w_qkv_bytes, w_qkv_scale, cos, sin, out_0, out_1, out_2):
@@ -54,7 +55,8 @@ def tile_quantllamaattentionfused_pa_kernel(tc, x, w_qkv_bytes, w_qkv_scale, cos
         wb_pool = ctx.enter_context(tc.tile_pool(name="wbytes", bufs=UNITS))
         wide_pool = ctx.enter_context(tc.tile_pool(name="wide", bufs=6))
         grp_pool = ctx.enter_context(tc.tile_pool(name="grp", bufs=2))
-        code_pool = ctx.enter_context(tc.tile_pool(name="codes", bufs=8))
+        head_pool = ctx.enter_context(tc.tile_pool(name="head", bufs=PASSES))
+        code_pool = ctx.enter_context(tc.tile_pool(name="codes", bufs=10))
         rope_pool = ctx.enter_context(tc.tile_pool(name="rope", bufs=5))
         res_pool = ctx.enter_context(tc.tile_pool(name="res", bufs=8))
         psum = ctx.enter_context(tc.psum_pool(name="psum", bufs=6))
@@ -73,6 +75,10 @@ def tile_quantllamaattentionfused_pa_kernel(tc, x, w_qkv_bytes, w_qkv_scale, cos
         sin_in = const.tile([P, TOKEN_TILES, HEAD // 2], BF16, name="sin_in")
         nc.scalar.dma_start(out=sin_in[:], in_=sin.rearrange("(m p) j -> p m j", p=P))
 
+        warm = const.tile([P, 2], F32, name="warm")
+        nc.vector.memset(warm[:], 0.0)
+        nc.scalar.activation(out=warm[:, 1:2], in_=warm[:, 0:1], func=COPY)
+
         w_bytes = []
         x_in = []
         for u in range(UNITS):
@@ -84,18 +90,20 @@ def tile_quantllamaattentionfused_pa_kernel(tc, x, w_qkv_bytes, w_qkv_scale, cos
             else:
                 nc.sync.dma_start(out=wb[:], in_=w_view[g][:, :, c * CHUNK : (c + 1) * CHUNK])
             w_bytes.append(wb)
-            if u < TOKEN_TILES:
+            if 1 <= u <= TOKEN_TILES:
                 xi = xin_pool.tile([P, HIDDEN], BF16, name="xi", tag="xi")
-                nc.sync.dma_start(out=xi[:], in_=x_rows[u * P : (u + 1) * P, :])
+                nc.sync.dma_start(out=xi[:], in_=x_rows[(u - 1) * P : u * P, :])
                 x_in.append(xi)
 
         tables = const.tile([P, TOKEN_TILES, 2, HEAD], F32, name="tables")
         cos2_v = tables[:, :, 0, :].rearrange("p m (j e) -> p m j e", e=2)
         sin2_v = tables[:, :, 1, :].rearrange("p m (j e) -> p m j e", e=2)
-        nc.vector.tensor_copy(out=cos2_v[:, :, :, 0], in_=cos_in[:])
-        nc.vector.tensor_copy(out=cos2_v[:, :, :, 1], in_=cos_in[:])
-        nc.vector.tensor_copy(out=sin2_v[:, :, :, 0], in_=sin_in[:])
-        nc.vector.tensor_scalar(out=sin2_v[:, :, :, 1], in0=sin_in[:], scalar1=-1.0, scalar2=None, op0=MULT)
+
+        def build_tables():
+            shape = [P, TOKEN_TILES, HEAD // 2, 2]
+            nc.vector.tensor_copy(out=cos2_v, in_=cos_in[:].unsqueeze(3).to_broadcast(shape))
+            nc.vector.tensor_copy(out=sin2_v[:, :, :, 0], in_=sin_in[:])
+            nc.vector.tensor_scalar(out=sin2_v[:, :, :, 1], in0=sin_in[:], scalar1=-1.0, scalar2=None, op0=MULT)
 
         wide = {}
         passed = {}
@@ -107,14 +115,34 @@ def tile_quantllamaattentionfused_pa_kernel(tc, x, w_qkv_bytes, w_qkv_scale, cos
         acc = {}
         prod = {}
 
-        def widen(u):
+        def wide_tile(u):
+            if u not in wide:
+                wd = wide_pool.tile([P, PACK, CHUNK], BF16, name="wd", tag="wd")
+                wide[u] = wd
+            return wide[u]
+
+        def planes_v(u):
+            return VECTOR_PLANES[u] if u < PASSES else 0
+
+        def widen_s(u):
             g = u % PASSES
-            wd = wide_pool.tile([P, PACK, CHUNK], BF16, name="wd", tag="wd")
-            for t in range(PACK):
+            wd = wide_tile(u)
+            for t in range(PACK - planes_v(u)):
                 nc.scalar.activation(
                     out=wd[:, t, :], in_=w_bytes[u][:, t, :].bitcast(FP8), func=COPY, scale=w_scale[:, g, t : t + 1]
                 )
-            wide[u] = wd
+
+        def widen_v(u):
+            g = u % PASSES
+            wd = wide_tile(u)
+            for t in range(PACK - planes_v(u), PACK):
+                nc.vector.tensor_scalar(
+                    out=wd[:, t, :],
+                    in0=w_bytes[u][:, t, :].bitcast(FP8),
+                    scalar1=w_scale[:, g, t : t + 1],
+                    scalar2=None,
+                    op0=MULT,
+                )
 
         def pass_through(u):
             pil = psum_il.tile([P, 2 * CHUNK], BF16, name="pil", tag="pil")
@@ -131,21 +159,24 @@ def tile_quantllamaattentionfused_pa_kernel(tc, x, w_qkv_bytes, w_qkv_scale, cos
 
         def group(u):
             if u not in grouped:
-                gr = grp_pool.tile([P, CHUNK, PACK], BF16, name="gr", tag="gr", align_bytes=64)
+                if u < PASSES:
+                    gr = head_pool.tile([P, CHUNK, PACK], BF16, name="gh", tag="gh", align_bytes=64)
+                else:
+                    gr = grp_pool.tile([P, CHUNK, PACK], BF16, name="gr", tag="gr", align_bytes=64)
                 grouped[u] = gr
             return grouped[u]
 
-        def bounds(u):
-            s_cols = scalar_cols(u)
-            v_end = CHUNK - s_cols - (LAST_GPSIMD_COLS if u == UNITS - 1 else GPSIMD_COLS)
-            return v_end, CHUNK - s_cols
+        def split(u):
+            if u < PASSES:
+                return CHUNK - HEAD_GPSIMD_COLS
+            return CHUNK - (LAST_GPSIMD_COLS if u == UNITS - 1 else GPSIMD_COLS)
 
         def interleave_g(u):
             gr = group(u)
-            a, b = bounds(u)
+            a = split(u)
             nc.gpsimd.tensor_scalar(
-                out=gr[:, a:b, :],
-                in0=wide[u][:, :, a:b].rearrange("p t n -> p n t"),
+                out=gr[:, a:, :],
+                in0=wide[u][:, :, a:].rearrange("p t n -> p n t"),
                 scalar1=1.0,
                 scalar2=0.0,
                 op0=MULT,
@@ -154,20 +185,16 @@ def tile_quantllamaattentionfused_pa_kernel(tc, x, w_qkv_bytes, w_qkv_scale, cos
 
         def interleave_s(u):
             gr = group(u)
-            cut = bounds(u)[1]
             nc.scalar.copy(
                 out=gr[:, :TENSOR_COLS, :].rearrange("p n t -> p (n t)"), in_=passed[u][:, : TENSOR_COLS * PACK]
             )
-            if cut < CHUNK:
-                nc.scalar.copy(out=gr[:, cut:, :], in_=wide[u][:, :, cut:].rearrange("p t n -> p n t"))
 
         def interleave_v(u):
             gr = group(u)
-            v_end = bounds(u)[0]
-            if v_end > TENSOR_COLS:
-                nc.vector.tensor_copy(
-                    out=gr[:, TENSOR_COLS:v_end, :], in_=wide[u][:, :, TENSOR_COLS:v_end].rearrange("p t n -> p n t")
-                )
+            a = split(u)
+            nc.vector.tensor_copy(
+                out=gr[:, TENSOR_COLS:a, :], in_=wide[u][:, :, TENSOR_COLS:a].rearrange("p t n -> p n t")
+            )
 
         def quantize_w(u):
             wc = code_pool.tile([P, CHUNK], U32, name="wc", tag="wc", align_bytes=64)
@@ -189,15 +216,17 @@ def tile_quantllamaattentionfused_pa_kernel(tc, x, w_qkv_bytes, w_qkv_scale, cos
                 banks.append(xt)
             x_banks[m] = banks
 
-        def x_copies(m):
-            xg = xq_pool.tile([P, PASSES * P * PACK], BF16, name="xg", tag="xg", align_bytes=64)
-            xg_words = xg[:].bitcast(F32).rearrange("p (g r u) -> p g r u", g=PASSES, u=2)
-            for half in range(2):
-                nc.vector.tensor_copy(
-                    out=xg_words[:, 2 * half : 2 * half + 2],
-                    in_=x_banks[m][half][:].rearrange("p (g u r) -> p g r u", g=2, u=2),
-                )
-            x_grouped[m] = xg
+        def x_copy(m, half, on_scalar):
+            if m not in x_grouped:
+                xg = xq_pool.tile([P, PASSES * P * PACK], BF16, name="xg", tag="xg", align_bytes=64)
+                x_grouped[m] = xg
+            xg_words = x_grouped[m][:].bitcast(F32).rearrange("p (g r u) -> p g r u", g=PASSES, u=2)
+            out = xg_words[:, 2 * half : 2 * half + 2]
+            bank = x_banks[m][half][:].rearrange("p (g u r) -> p g r u", g=2, u=2)
+            if on_scalar:
+                nc.scalar.copy(out=out, in_=bank)
+            else:
+                nc.vector.tensor_copy(out=out, in_=bank)
 
         def quantize_x(m):
             xc = xq_pool.tile([P, PASSES * P], U32, name="xc", tag="xc", align_bytes=64)
@@ -253,77 +282,103 @@ def tile_quantllamaattentionfused_pa_kernel(tc, x, w_qkv_bytes, w_qkv_scale, cos
                 nc.vector.tensor_copy(out=res[:], in_=acc[(c, m)][:])
             nc.sync.dma_start(out=out_block(c, m), in_=res[:])
 
-        def scalar_cols(u):
-            return 0
-
         def piece_of(i):
             return i // TOKEN_TILES, i % TOKEN_TILES
 
         PIECES = ROPE_CHUNKS * TOKEN_TILES
 
-        x_transposes(0)
-        x_transposes(1)
-        widen(0)
-        pass_through(0)
-        widen(1)
-        pass_through(1)
-        interleave_g(0)
-        interleave_s(0)
-        x_copies(0)
-        interleave_v(0)
-        x_transposes(2)
-        widen(2)
-        pass_through(2)
-        interleave_g(1)
-        interleave_s(1)
-        quantize_x(0)
-        x_copies(1)
-        interleave_v(1)
+        def tile_passes(c, m):
+            for g in range(PASSES):
+                multiply(c * PASSES + g, m)
 
-        for tick in range(UNITS - 1):
-            piece = tick - (PASSES - 1)
-            if tick == 0:
-                x_transposes(3)
+        def late_passes(g):
+            for m in range(TOKEN_TILES):
+                multiply((CHUNKS - 1) * PASSES + g, m)
+
+        widen_s(0)
+        widen_v(0)
+        widen_s(1)
+        widen_v(1)
+        pass_through(0)
+        x_transposes(0)
+        pass_through(1)
+        interleave_v(0)
+        interleave_s(0)
+        widen_s(2)
+        x_copy(0, 0, True)
+        x_copy(0, 1, True)
+        interleave_s(1)
+        quantize_w(0)
+        widen_v(2)
+        interleave_v(1)
+        x_transposes(1)
+        pass_through(2)
+        quantize_x(0)
+        quantize_w(1)
+        widen_s(3)
+        x_copy(1, 0, True)
+        x_copy(1, 1, True)
+        interleave_s(2)
+        widen_v(3)
+        interleave_v(2)
+        x_transposes(2)
+        pass_through(3)
+        quantize_x(1)
+        quantize_w(2)
+        x_copy(2, 0, True)
+        x_copy(2, 1, True)
+        interleave_s(3)
+        interleave_v(3)
+        x_transposes(3)
+        widen_s(4)
+        quantize_x(2)
+        quantize_w(3)
+        x_copy(3, 0, False)
+        x_copy(3, 1, False)
+        pass_through(4)
+        for m in range(TOKEN_TILES - 1):
+            for g in range(PASSES):
+                multiply(g, m)
+        build_tables()
+        quantize_x(3)
+        interleave_g(4)
+        rope_products(0, 0)
+        widen_s(5)
+        interleave_s(4)
+        pass_through(5)
+        for g in range(PASSES):
+            multiply(g, TOKEN_TILES - 1)
+        interleave_v(4)
+        interleave_g(5)
+        widen_s(6)
+        pass_through(6)
+
+        for tick in range(PASSES, UNITS):
+            piece = tick - PASSES
+            if tick < 2 * PASSES:
+                piece += 1
             if tick + 3 < UNITS:
-                widen(tick + 3)
+                widen_s(tick + 3)
+            if tick + 1 < UNITS:
+                interleave_v(tick + 1)
+                interleave_s(tick + 1)
+            if tick != 2 * PASSES:
+                rope_sum(*piece_of(piece - 1))
             quantize_w(tick)
-            if tick == UNITS - 2:
-                quantize_w(tick + 1)
             if tick + 2 < UNITS:
                 interleave_g(tick + 2)
-            if tick > PASSES - 2:
-                multiply(tick, 0)
-            if tick == UNITS - 2:
-                for m in range(1, TOKEN_TILES):
-                    multiply(tick, m)
-                for m in range(TOKEN_TILES):
-                    multiply(tick + 1, m)
-            if piece < 0:
-                interleave_v(tick + 2)
-            if 1 <= piece <= PIECES:
-                rope_sum(*piece_of(piece - 1))
-            if tick + 2 < TOKEN_TILES:
-                x_copies(tick + 2)
-            early_copy = piece >= 0 and piece % TOKEN_TILES == 0 and tick + 2 < UNITS
-            if early_copy:
-                interleave_v(tick + 2)
-            if 0 <= piece < PIECES:
-                rope_products(*piece_of(piece))
-            if tick + 1 < TOKEN_TILES:
-                quantize_x(tick + 1)
-            if tick == PASSES - 2:
-                for g in range(PASSES - 1):
-                    for m in range(TOKEN_TILES):
-                        multiply(g, m)
-            if tick > PASSES - 2 and tick < UNITS - 2:
-                for m in range(1, TOKEN_TILES):
-                    multiply(tick, m)
+            if TOKEN_TILES <= tick - PASSES + 1 < PIECES:
+                tile_passes(*piece_of(tick - PASSES + 1))
             if tick + 3 < UNITS:
                 pass_through(tick + 3)
-            if tick + 2 < UNITS:
-                interleave_s(tick + 2)
-                if piece >= 0 and not early_copy:
-                    interleave_v(tick + 2)
+            if tick != 2 * PASSES - 1:
+                rope_products(*piece_of(piece))
+            if tick == UNITS - 3:
+                late_passes(0)
+            if tick == UNITS - 2:
+                late_passes(1)
+                late_passes(2)
+        late_passes(3)
         for m in range(TOKEN_TILES):
             plain_copy(CHUNKS - 1, m, True)
         rope_sum(ROPE_CHUNKS - 1, TOKEN_TILES - 1)

@@ -186,7 +186,8 @@ def tile_quantllamaattentionfused_pa_kernel(tc, x, w_qkv_bytes, w_qkv_scale, cos
         def interleave_s(u):
             gr = group(u)
             nc.scalar.copy(
-                out=gr[:, :TENSOR_COLS, :].rearrange("p n t -> p (n t)"), in_=passed[u][:, : TENSOR_COLS * PACK]
+                out=gr[:, :TENSOR_COLS, :].rearrange("p n t -> p (n t)").bitcast(F32),
+                in_=passed[u][:, : TENSOR_COLS * PACK].bitcast(F32),
             )
 
         def interleave_v(u):

@@ -29,6 +29,7 @@ TENSOR_COLS = 192
 GPSIMD_COLS = 192
 LAST_GPSIMD_COLS = 128
 HEAD_GPSIMD_COLS = 0
+RUN = 4
 VECTOR_PLANES = (2, 2, 2, 2)
 
 
@@ -194,7 +195,8 @@ def tile_quantllamaattentionfused_pa_kernel(tc, x, w_qkv_bytes, w_qkv_scale, cos
             gr = group(u)
             a = split(u)
             nc.vector.tensor_copy(
-                out=gr[:, TENSOR_COLS:a, :], in_=wide[u][:, :, TENSOR_COLS:a].rearrange("p t n -> p n t")
+                out=gr[:, TENSOR_COLS:a, :].rearrange("p (c i) t -> p c t i", i=RUN),
+                in_=wide[u][:, :, TENSOR_COLS:a].rearrange("p t (c i) -> p c t i", i=RUN),
             )
 
         def quantize_w(u):

@@ -26,7 +26,7 @@ ROPE_CHUNKS = 5
 UNITS = CHUNKS * PASSES
 HEAD = 128
 TENSOR_COLS = 192
-GPSIMD_COLS = 192
+GPSIMD_COLS = 176
 LAST_GPSIMD_COLS = 128
 HEAD_GPSIMD_COLS = 0
 RUN = 4
@@ -55,7 +55,7 @@ def tile_quantllamaattentionfused_pa_kernel(tc, x, w_qkv_bytes, w_qkv_scale, cos
         xq_pool = ctx.enter_context(tc.tile_pool(name="xq", bufs=TOKEN_TILES))
         wb_pool = ctx.enter_context(tc.tile_pool(name="wbytes", bufs=UNITS))
         wide_pool = ctx.enter_context(tc.tile_pool(name="wide", bufs=6))
-        grp_pool = ctx.enter_context(tc.tile_pool(name="grp", bufs=2))
+        grp_pool = ctx.enter_context(tc.tile_pool(name="grp", bufs=3))
         head_pool = ctx.enter_context(tc.tile_pool(name="head", bufs=PASSES))
         code_pool = ctx.enter_context(tc.tile_pool(name="codes", bufs=10))
         rope_pool = ctx.enter_context(tc.tile_pool(name="rope", bufs=5))
@@ -194,6 +194,8 @@ def tile_quantllamaattentionfused_pa_kernel(tc, x, w_qkv_bytes, w_qkv_scale, cos
         def interleave_v(u):
             gr = group(u)
             a = split(u)
+            if a < CHUNK:
+                a += RUN
             nc.vector.tensor_copy(
                 out=gr[:, TENSOR_COLS:a, :].rearrange("p (c i) t -> p c t i", i=RUN),
                 in_=wide[u][:, :, TENSOR_COLS:a].rearrange("p t (c i) -> p c t i", i=RUN),
@@ -344,6 +346,7 @@ def tile_quantllamaattentionfused_pa_kernel(tc, x, w_qkv_bytes, w_qkv_scale, cos
                 multiply(g, m)
         build_tables()
         quantize_x(3)
+        interleave_v(4)
         interleave_g(4)
         rope_products(0, 0)
         widen_s(5)
@@ -351,11 +354,12 @@ def tile_quantllamaattentionfused_pa_kernel(tc, x, w_qkv_bytes, w_qkv_scale, cos
         pass_through(5)
         for g in range(PASSES):
             multiply(g, TOKEN_TILES - 1)
-        interleave_v(4)
+        interleave_v(5)
         interleave_g(5)
         widen_s(6)
         pass_through(6)
 
+        pending = [0]
         for tick in range(PASSES, UNITS):
             piece = tick - PASSES
             if tick < 2 * PASSES:
@@ -363,19 +367,20 @@ def tile_quantllamaattentionfused_pa_kernel(tc, x, w_qkv_bytes, w_qkv_scale, cos
             if tick + 3 < UNITS:
                 widen_s(tick + 3)
             if tick + 1 < UNITS:
-                interleave_v(tick + 1)
                 interleave_s(tick + 1)
-            if tick != 2 * PASSES:
-                rope_sum(*piece_of(piece - 1))
-            quantize_w(tick)
+            if len(pending) > 1 or tick == 2 * PASSES - 1:
+                rope_sum(*piece_of(pending.pop(0)))
             if tick + 2 < UNITS:
+                interleave_v(tick + 2)
                 interleave_g(tick + 2)
+            quantize_w(tick)
             if TOKEN_TILES <= tick - PASSES + 1 < PIECES:
                 tile_passes(*piece_of(tick - PASSES + 1))
             if tick + 3 < UNITS:
                 pass_through(tick + 3)
             if tick != 2 * PASSES - 1:
                 rope_products(*piece_of(piece))
+                pending.append(piece)
             if tick == UNITS - 3:
                 late_passes(0)
             if tick == UNITS - 2:
@@ -384,4 +389,5 @@ def tile_quantllamaattentionfused_pa_kernel(tc, x, w_qkv_bytes, w_qkv_scale, cos
         late_passes(3)
         for m in range(TOKEN_TILES):
             plain_copy(CHUNKS - 1, m, True)
-        rope_sum(ROPE_CHUNKS - 1, TOKEN_TILES - 1)
+        for piece in pending:
+            rope_sum(*piece_of(piece))

@@ -25,12 +25,12 @@ CHUNKS = FEATURES // CHUNK
 ROPE_CHUNKS = 5
 UNITS = CHUNKS * PASSES
 HEAD = 128
-TENSOR_COLS = 192
+TENSOR_COLS = 144
 GPSIMD_COLS = 176
-LAST_GPSIMD_COLS = 128
+LAST_GPSIMD_COLS = 0
 HEAD_GPSIMD_COLS = 0
 RUN = 4
-VECTOR_PLANES = (2, 2, 2, 2)
+VECTOR_PLANES = (2, 1, 1, 1)
 
 
 def tile_quantllamaattentionfused_pa_kernel(tc, x, w_qkv_bytes, w_qkv_scale, cos, sin, out_0, out_1, out_2):
@@ -285,7 +285,7 @@ def tile_quantllamaattentionfused_pa_kernel(tc, x, w_qkv_bytes, w_qkv_scale, cos
                 nc.scalar.copy(out=res[:], in_=acc[(c, m)][:])
             else:
                 nc.vector.tensor_copy(out=res[:], in_=acc[(c, m)][:])
-            nc.sync.dma_start(out=out_block(c, m), in_=res[:])
+            nc.scalar.dma_start(out=out_block(c, m), in_=res[:])
 
         def piece_of(i):
             return i // TOKEN_TILES, i % TOKEN_TILES
@@ -300,8 +300,8 @@ def tile_quantllamaattentionfused_pa_kernel(tc, x, w_qkv_bytes, w_qkv_scale, cos
             for m in range(TOKEN_TILES):
                 multiply((CHUNKS - 1) * PASSES + g, m)
 
-        widen_s(0)
         widen_v(0)
+        widen_s(0)
         widen_s(1)
         widen_v(1)
         pass_through(0)
@@ -318,6 +318,7 @@ def tile_quantllamaattentionfused_pa_kernel(tc, x, w_qkv_bytes, w_qkv_scale, cos
         interleave_v(1)
         x_transposes(1)
         pass_through(2)
+        build_tables()
         quantize_x(0)
         quantize_w(1)
         widen_s(3)
@@ -335,59 +336,60 @@ def tile_quantllamaattentionfused_pa_kernel(tc, x, w_qkv_bytes, w_qkv_scale, cos
         interleave_s(3)
         interleave_v(3)
         x_transposes(3)
+        for m in range(TOKEN_TILES - 2):
+            for g in range(PASSES - 1):
+                multiply(g, m)
         widen_s(4)
         quantize_x(2)
         quantize_w(3)
+        multiply(PASSES - 1, 0)
+        multiply(PASSES - 1, 1)
+        for g in range(PASSES):
+            multiply(g, TOKEN_TILES - 2)
+        pass_through(4)
         x_copy(3, 0, False)
         x_copy(3, 1, False)
-        pass_through(4)
-        for m in range(TOKEN_TILES - 1):
-            for g in range(PASSES):
-                multiply(g, m)
-        build_tables()
-        quantize_x(3)
         interleave_v(4)
         interleave_g(4)
         rope_products(0, 0)
+        quantize_x(3)
+        for g in range(PASSES):
+            multiply(g, TOKEN_TILES - 1)
         widen_s(5)
         interleave_s(4)
         pass_through(5)
-        for g in range(PASSES):
-            multiply(g, TOKEN_TILES - 1)
-        interleave_v(5)
-        interleave_g(5)
-        widen_s(6)
-        pass_through(6)
-
         pending = [0]
         for tick in range(PASSES, UNITS):
             piece = tick - PASSES
             if tick < 2 * PASSES:
                 piece += 1
-            if tick + 3 < UNITS:
-                widen_s(tick + 3)
+            products = tick != 2 * PASSES - 1
+            if tick + 2 < UNITS:
+                widen_s(tick + 2)
             if tick + 1 < UNITS:
                 interleave_s(tick + 1)
-            if len(pending) > 1 or tick == 2 * PASSES - 1:
+            if len(pending) > 1 or not products:
                 rope_sum(*piece_of(pending.pop(0)))
-            if tick + 2 < UNITS:
-                interleave_v(tick + 2)
-                interleave_g(tick + 2)
-            quantize_w(tick)
+            if tick + 1 < UNITS:
+                interleave_v(tick + 1)
+                if tick + 1 < UNITS - 1:
+                    interleave_g(tick + 1)
+            if tick < UNITS - 1:
+                quantize_w(tick)
+            if tick == UNITS - 2:
+                quantize_w(tick + 1)
             if TOKEN_TILES <= tick - PASSES + 1 < PIECES:
                 tile_passes(*piece_of(tick - PASSES + 1))
-            if tick + 3 < UNITS:
-                pass_through(tick + 3)
-            if tick != 2 * PASSES - 1:
+            if tick >= UNITS - PASSES and tick < UNITS - 1:
+                late_passes(tick - UNITS + PASSES)
+            if tick + 2 < UNITS:
+                pass_through(tick + 2)
+            if tick == UNITS - 2:
+                late_passes(PASSES - 1)
+                for m in range(TOKEN_TILES):
+                    plain_copy(CHUNKS - 1, m, True)
+            if products:
                 rope_products(*piece_of(piece))
                 pending.append(piece)
-            if tick == UNITS - 3:
-                late_passes(0)
-            if tick == UNITS - 2:
-                late_passes(1)
-                late_passes(2)
-        late_passes(3)
-        for m in range(TOKEN_TILES):
-            plain_copy(CHUNKS - 1, m, True)
         for piece in pending:
             rope_sum(*piece_of(piece))

@@ -24,11 +24,11 @@ CHUNK = 512
 CHUNKS = FEATURES // CHUNK
 ROPE_CHUNKS = 5
 UNITS = CHUNKS * PASSES
+PIECES = ROPE_CHUNKS * TOKEN_TILES
 HEAD = 128
-TENSOR_COLS = 144
-GPSIMD_COLS = 176
-LAST_GPSIMD_COLS = 0
-HEAD_GPSIMD_COLS = 0
+
+TENSOR_COLS = 176
+GPSIMD_COLS = 184
 RUN = 4
 VECTOR_PLANES = (2, 1, 1, 1)
 
@@ -43,23 +43,25 @@ def tile_quantllamaattentionfused_pa_kernel(tc, x, w_qkv_bytes, w_qkv_scale, cos
 
     def out_block(c, m):
         rows = slice(m * P, (m + 1) * P)
-        if c < 4:
+        if c < ROPE_CHUNKS - 1:
             return q_rows[rows, c * CHUNK : (c + 1) * CHUNK]
-        if c == 4:
-            return k_rows[rows, :]
-        return v_rows[rows, :]
+        return (k_rows if c < ROPE_CHUNKS else v_rows)[rows, :]
+
+    def piece_of(piece):
+        return divmod(piece, TOKEN_TILES)
 
     with ExitStack() as ctx:
         const = ctx.enter_context(tc.tile_pool(name="const", bufs=1))
         xin_pool = ctx.enter_context(tc.tile_pool(name="xin", bufs=TOKEN_TILES))
         xq_pool = ctx.enter_context(tc.tile_pool(name="xq", bufs=TOKEN_TILES))
-        wb_pool = ctx.enter_context(tc.tile_pool(name="wbytes", bufs=UNITS))
+        wb_pool = ctx.enter_context(tc.tile_pool(name="wbytes", bufs=2 * PASSES))
         wide_pool = ctx.enter_context(tc.tile_pool(name="wide", bufs=6))
-        grp_pool = ctx.enter_context(tc.tile_pool(name="grp", bufs=3))
         head_pool = ctx.enter_context(tc.tile_pool(name="head", bufs=PASSES))
+        grp_pool = ctx.enter_context(tc.tile_pool(name="grp", bufs=3))
         code_pool = ctx.enter_context(tc.tile_pool(name="codes", bufs=10))
         rope_pool = ctx.enter_context(tc.tile_pool(name="rope", bufs=5))
-        res_pool = ctx.enter_context(tc.tile_pool(name="res", bufs=8))
+        res_pool = ctx.enter_context(tc.tile_pool(name="res", bufs=4))
+        val_pool = ctx.enter_context(tc.tile_pool(name="val", bufs=TOKEN_TILES))
         psum = ctx.enter_context(tc.psum_pool(name="psum", bufs=6))
         psum_il = ctx.enter_context(tc.psum_pool(name="psum_il", bufs=2))
         ctx.enter_context(tc.manual_schedule())
@@ -80,31 +82,26 @@ def tile_quantllamaattentionfused_pa_kernel(tc, x, w_qkv_bytes, w_qkv_scale, cos
         nc.vector.memset(warm[:], 0.0)
         nc.scalar.activation(out=warm[:, 1:2], in_=warm[:, 0:1], func=COPY)
 
-        w_bytes = []
+        w_bytes = {}
         x_in = []
-        for u in range(UNITS):
-            c, g = divmod(u, PASSES)
-            wb = wb_pool.tile([P, PACK, CHUNK], U8, name="wb", tag="wb")
-            if u == 0:
-                for t in range(PACK):
-                    nc.sync.dma_start(out=wb[:, t, :], in_=w_view[g][:, t, :CHUNK])
-            else:
-                nc.sync.dma_start(out=wb[:], in_=w_view[g][:, :, c * CHUNK : (c + 1) * CHUNK])
-            w_bytes.append(wb)
-            if 1 <= u <= TOKEN_TILES:
-                xi = xin_pool.tile([P, HIDDEN], BF16, name="xi", tag="xi")
-                nc.sync.dma_start(out=xi[:], in_=x_rows[(u - 1) * P : u * P, :])
-                x_in.append(xi)
+        for c, width in ((0, 1), (1, 2), (3, 2), (5, 1)):
+            for g in range(PASSES):
+                wb = wb_pool.tile([P, PACK, width * CHUNK], U8, name="wb", tag="wb%d" % width)
+                for i in range(width):
+                    w_bytes[(c + i) * PASSES + g] = wb[:, :, i * CHUNK : (i + 1) * CHUNK]
+                source = w_view[g][:, :, c * CHUNK : (c + width) * CHUNK]
+                if c == 0 and g == 0:
+                    for t in range(PACK):
+                        nc.sync.dma_start(out=wb[:, t, :], in_=source[:, t, :])
+                else:
+                    nc.sync.dma_start(out=wb[:], in_=source)
+                if (c == 0 and g > 0) or (c == 1 and g == 0):
+                    m = len(x_in)
+                    xi = xin_pool.tile([P, HIDDEN], BF16, name="xi", tag="xi")
+                    nc.sync.dma_start(out=xi[:], in_=x_rows[m * P : (m + 1) * P, :])
+                    x_in.append(xi)
 
         tables = const.tile([P, TOKEN_TILES, 2, HEAD], F32, name="tables")
-        cos2_v = tables[:, :, 0, :].rearrange("p m (j e) -> p m j e", e=2)
-        sin2_v = tables[:, :, 1, :].rearrange("p m (j e) -> p m j e", e=2)
-
-        def build_tables():
-            shape = [P, TOKEN_TILES, HEAD // 2, 2]
-            nc.vector.tensor_copy(out=cos2_v, in_=cos_in[:].unsqueeze(3).to_broadcast(shape))
-            nc.vector.tensor_copy(out=sin2_v[:, :, :, 0], in_=sin_in[:])
-            nc.vector.tensor_scalar(out=sin2_v[:, :, :, 1], in0=sin_in[:], scalar1=-1.0, scalar2=None, op0=MULT)
 
         wide = {}
         passed = {}
@@ -116,43 +113,46 @@ def tile_quantllamaattentionfused_pa_kernel(tc, x, w_qkv_bytes, w_qkv_scale, cos
         acc = {}
         prod = {}
 
+        def build_tables():
+            cos2 = tables[:, :, 0, :].rearrange("p m (j e) -> p m j e", e=2)
+            sin2 = tables[:, :, 1, :].rearrange("p m (j e) -> p m j e", e=2)
+            cos_pairs = cos_in[:].unsqueeze(3).to_broadcast([P, TOKEN_TILES, HEAD // 2, 2])
+            nc.vector.tensor_copy(out=cos2, in_=cos_pairs)
+            nc.vector.tensor_copy(out=sin2[:, :, :, 0], in_=sin_in[:])
+            nc.vector.tensor_scalar(out=sin2[:, :, :, 1], in0=sin_in[:], scalar1=-1.0, scalar2=None, op0=MULT)
+
         def wide_tile(u):
             if u not in wide:
                 wd = wide_pool.tile([P, PACK, CHUNK], BF16, name="wd", tag="wd")
                 wide[u] = wd
             return wide[u]
 
-        def planes_v(u):
-            return VECTOR_PLANES[u] if u < PASSES else 0
-
-        def widen_s(u):
-            g = u % PASSES
-            wd = wide_tile(u)
-            for t in range(PACK - planes_v(u)):
-                nc.scalar.activation(
-                    out=wd[:, t, :], in_=w_bytes[u][:, t, :].bitcast(FP8), func=COPY, scale=w_scale[:, g, t : t + 1]
-                )
-
         def widen_v(u):
-            g = u % PASSES
-            wd = wide_tile(u)
-            for t in range(PACK - planes_v(u), PACK):
+            for t in range(PACK - VECTOR_PLANES[u], PACK):
                 nc.vector.tensor_scalar(
-                    out=wd[:, t, :],
+                    out=wide_tile(u)[:, t, :],
                     in0=w_bytes[u][:, t, :].bitcast(FP8),
-                    scalar1=w_scale[:, g, t : t + 1],
+                    scalar1=w_scale[:, u % PASSES, t : t + 1],
                     scalar2=None,
                     op0=MULT,
                 )
 
+        def widen_s(u):
+            for t in range(PACK - (VECTOR_PLANES[u] if u < PASSES else 0)):
+                nc.scalar.activation(
+                    out=wide_tile(u)[:, t, :],
+                    in_=w_bytes[u][:, t, :].bitcast(FP8),
+                    func=COPY,
+                    scale=w_scale[:, u % PASSES, t : t + 1],
+                )
+
         def pass_through(u):
-            pil = psum_il.tile([P, 2 * CHUNK], BF16, name="pil", tag="pil")
-            wd = wide[u]
+            pil = psum_il.tile([P, CHUNK * 2], BF16, name="pil", tag="pil")
             for n0, n1 in ((0, 128), (128, TENSOR_COLS)):
                 nc.tensor.matmul(
                     out=pil[:, n0 * PACK : n1 * PACK].rearrange("p (n t) -> p n t", t=PACK),
                     lhsT=ident_bf[:],
-                    rhs=wd[:, :, n0:n1].rearrange("p t n -> p n t"),
+                    rhs=wide[u][:, :, n0:n1].rearrange("p t n -> p n t"),
                     start=True,
                     stop=True,
                 )
@@ -167,39 +167,32 @@ def tile_quantllamaattentionfused_pa_kernel(tc, x, w_qkv_bytes, w_qkv_scale, cos
                 grouped[u] = gr
             return grouped[u]
 
-        def split(u):
-            if u < PASSES:
-                return CHUNK - HEAD_GPSIMD_COLS
-            return CHUNK - (LAST_GPSIMD_COLS if u == UNITS - 1 else GPSIMD_COLS)
-
-        def interleave_g(u):
-            gr = group(u)
-            a = split(u)
-            nc.gpsimd.tensor_scalar(
-                out=gr[:, a:, :],
-                in0=wide[u][:, :, a:].rearrange("p t n -> p n t"),
-                scalar1=1.0,
-                scalar2=0.0,
-                op0=MULT,
-                op1=ADD,
-            )
+        def gpsimd_cols(u):
+            return GPSIMD_COLS if PASSES <= u < UNITS - 1 else 0
 
         def interleave_s(u):
-            gr = group(u)
             nc.scalar.copy(
-                out=gr[:, :TENSOR_COLS, :].rearrange("p n t -> p (n t)").bitcast(F32),
+                out=group(u)[:, :TENSOR_COLS, :].rearrange("p n t -> p (n t)").bitcast(F32),
                 in_=passed[u][:, : TENSOR_COLS * PACK].bitcast(F32),
             )
 
-        def interleave_v(u):
+        def interleave(u):
             gr = group(u)
-            a = split(u)
-            if a < CHUNK:
-                a += RUN
+            cut = CHUNK - gpsimd_cols(u)
+            end = min(cut + RUN, CHUNK)
             nc.vector.tensor_copy(
-                out=gr[:, TENSOR_COLS:a, :].rearrange("p (c i) t -> p c t i", i=RUN),
-                in_=wide[u][:, :, TENSOR_COLS:a].rearrange("p t (c i) -> p c t i", i=RUN),
+                out=gr[:, TENSOR_COLS:end, :].rearrange("p (c i) t -> p c t i", i=RUN),
+                in_=wide[u][:, :, TENSOR_COLS:end].rearrange("p t (c i) -> p c t i", i=RUN),
             )
+            if cut < CHUNK:
+                nc.gpsimd.tensor_scalar(
+                    out=gr[:, cut:, :],
+                    in0=wide[u][:, :, cut:].rearrange("p t n -> p n t"),
+                    scalar1=1.0,
+                    scalar2=0.0,
+                    op0=MULT,
+                    op1=ADD,
+                )
 
         def quantize_w(u):
             wc = code_pool.tile([P, CHUNK], U32, name="wc", tag="wc", align_bytes=64)
@@ -221,17 +214,15 @@ def tile_quantllamaattentionfused_pa_kernel(tc, x, w_qkv_bytes, w_qkv_scale, cos
                 banks.append(xt)
             x_banks[m] = banks
 
-        def x_copy(m, half, on_scalar):
-            if m not in x_grouped:
-                xg = xq_pool.tile([P, PASSES * P * PACK], BF16, name="xg", tag="xg", align_bytes=64)
-                x_grouped[m] = xg
-            xg_words = x_grouped[m][:].bitcast(F32).rearrange("p (g r u) -> p g r u", g=PASSES, u=2)
-            out = xg_words[:, 2 * half : 2 * half + 2]
-            bank = x_banks[m][half][:].rearrange("p (g u r) -> p g r u", g=2, u=2)
-            if on_scalar:
-                nc.scalar.copy(out=out, in_=bank)
-            else:
-                nc.vector.tensor_copy(out=out, in_=bank)
+        def x_copies(m, copy):
+            xg = xq_pool.tile([P, PASSES * P * PACK], BF16, name="xg", tag="xg", align_bytes=64)
+            xg_words = xg[:].bitcast(F32).rearrange("p (g r u) -> p g r u", g=PASSES, u=2)
+            for half in range(2):
+                copy(
+                    out=xg_words[:, 2 * half : 2 * half + 2],
+                    in_=x_banks[m][half][:].rearrange("p (g u r) -> p g r u", g=2, u=2),
+                )
+            x_grouped[m] = xg
 
         def quantize_x(m):
             xc = xq_pool.tile([P, PASSES * P], U32, name="xc", tag="xc", align_bytes=64)
@@ -239,25 +230,26 @@ def tile_quantllamaattentionfused_pa_kernel(tc, x, w_qkv_bytes, w_qkv_scale, cos
             nc.vector.quantize_mx(out=xc[:].bitcast(FP8X4), scales=xs[:], in_=x_grouped[m][:])
             x_codes[m] = (xc, xs)
 
-        def multiply(u, m):
-            c, g = divmod(u, PASSES)
-            if g == 0:
-                bank = psum.tile([P, CHUNK], F32, name="acc", tag="acc")
-                acc[(c, m)] = bank
-            xc, xs = x_codes[m]
-            wc, ws = w_codes[u]
-            cols = slice(g * P, (g + 1) * P)
-            nc.tensor.matmul_mx(
-                out=acc[(c, m)][:],
-                lhsT=xc[:, cols].bitcast(FP8X4),
-                lhsT_scale=xs[:, cols],
-                rhs=wc[:].bitcast(FP8X4),
-                rhs_scale=ws[:],
-                start=(g == 0),
-                stop=(g == PASSES - 1),
-            )
+        def multiply(c, m, passes):
+            for g in passes:
+                if g == 0:
+                    bank = psum.tile([P, CHUNK], F32, name="acc", tag="acc")
+                    acc[(c, m)] = bank
+                xc, xs = x_codes[m]
+                wc, ws = w_codes[c * PASSES + g]
+                cols = slice(g * P, (g + 1) * P)
+                nc.tensor.matmul_mx(
+                    out=acc[(c, m)][:],
+                    lhsT=xc[:, cols].bitcast(FP8X4),
+                    lhsT_scale=xs[:, cols],
+                    rhs=wc[:].bitcast(FP8X4),
+                    rhs_scale=ws[:],
+                    start=(g == 0),
+                    stop=(g == PASSES - 1),
+                )
 
-        def rope_products(c, m):
+        def rope_products(piece):
+            c, m = piece_of(piece)
             pab = rope_pool.tile([P, 2, CHUNK], F32, name="pab", tag="pab")
             shape = [P, 2, CHUNK // HEAD, HEAD]
             nc.vector.tensor_tensor(
@@ -266,39 +258,23 @@ def tile_quantllamaattentionfused_pa_kernel(tc, x, w_qkv_bytes, w_qkv_scale, cos
                 in1=tables[:, m, :, :].unsqueeze(2).to_broadcast(shape),
                 op=MULT,
             )
-            prod[(c, m)] = pab
+            prod[piece] = pab
 
-        def rope_sum(c, m):
-            pab = prod[(c, m)]
+        def rope_sum(piece, engine):
+            pab = prod[piece]
             res = res_pool.tile([P, CHUNK], F32, name="res", tag="res")
-            nc.vector.tensor_tensor(
+            engine.tensor_tensor(
                 out=res[:].rearrange("p (j e) -> p j e", e=2),
                 in0=pab[:, 0, :].rearrange("p (j e) -> p j e", e=2),
                 in1=pab[:, 1, :].rearrange("p (j e) -> p j e", e=2)[:, :, ::-1],
                 op=ADD,
             )
-            nc.sync.dma_start(out=out_block(c, m), in_=res[:])
+            nc.sync.dma_start(out=out_block(*piece_of(piece)), in_=res[:])
 
-        def plain_copy(c, m, on_scalar):
-            res = res_pool.tile([P, CHUNK], F32, name="res", tag="res")
-            if on_scalar:
-                nc.scalar.copy(out=res[:], in_=acc[(c, m)][:])
-            else:
-                nc.vector.tensor_copy(out=res[:], in_=acc[(c, m)][:])
-            nc.scalar.dma_start(out=out_block(c, m), in_=res[:])
-
-        def piece_of(i):
-            return i // TOKEN_TILES, i % TOKEN_TILES
-
-        PIECES = ROPE_CHUNKS * TOKEN_TILES
-
-        def tile_passes(c, m):
-            for g in range(PASSES):
-                multiply(c * PASSES + g, m)
-
-        def late_passes(g):
-            for m in range(TOKEN_TILES):
-                multiply((CHUNKS - 1) * PASSES + g, m)
+        def value_copy(m):
+            val = val_pool.tile([P, CHUNK], F32, name="val", tag="val")
+            nc.scalar.copy(out=val[:], in_=acc[(CHUNKS - 1, m)][:])
+            nc.scalar.dma_start(out=out_block(CHUNKS - 1, m), in_=val[:])
 
         widen_v(0)
         widen_s(0)
@@ -307,89 +283,74 @@ def tile_quantllamaattentionfused_pa_kernel(tc, x, w_qkv_bytes, w_qkv_scale, cos
         pass_through(0)
         x_transposes(0)
         pass_through(1)
-        interleave_v(0)
-        interleave_s(0)
-        widen_s(2)
-        x_copy(0, 0, True)
-        x_copy(0, 1, True)
-        interleave_s(1)
-        quantize_w(0)
-        widen_v(2)
-        interleave_v(1)
-        x_transposes(1)
-        pass_through(2)
-        build_tables()
-        quantize_x(0)
-        quantize_w(1)
-        widen_s(3)
-        x_copy(1, 0, True)
-        x_copy(1, 1, True)
-        interleave_s(2)
-        widen_v(3)
-        interleave_v(2)
-        x_transposes(2)
-        pass_through(3)
-        quantize_x(1)
-        quantize_w(2)
-        x_copy(2, 0, True)
-        x_copy(2, 1, True)
-        interleave_s(3)
-        interleave_v(3)
-        x_transposes(3)
-        for m in range(TOKEN_TILES - 2):
-            for g in range(PASSES - 1):
-                multiply(g, m)
-        widen_s(4)
-        quantize_x(2)
-        quantize_w(3)
-        multiply(PASSES - 1, 0)
-        multiply(PASSES - 1, 1)
-        for g in range(PASSES):
-            multiply(g, TOKEN_TILES - 2)
-        pass_through(4)
-        x_copy(3, 0, False)
-        x_copy(3, 1, False)
-        interleave_v(4)
-        interleave_g(4)
-        rope_products(0, 0)
-        quantize_x(3)
-        for g in range(PASSES):
-            multiply(g, TOKEN_TILES - 1)
-        widen_s(5)
-        interleave_s(4)
-        pass_through(5)
-        pending = [0]
-        for tick in range(PASSES, UNITS):
-            piece = tick - PASSES
-            if tick < 2 * PASSES:
-                piece += 1
-            products = tick != 2 * PASSES - 1
-            if tick + 2 < UNITS:
-                widen_s(tick + 2)
-            if tick + 1 < UNITS:
-                interleave_s(tick + 1)
-            if len(pending) > 1 or not products:
-                rope_sum(*piece_of(pending.pop(0)))
-            if tick + 1 < UNITS:
-                interleave_v(tick + 1)
-                if tick + 1 < UNITS - 1:
-                    interleave_g(tick + 1)
-            if tick < UNITS - 1:
-                quantize_w(tick)
-            if tick == UNITS - 2:
-                quantize_w(tick + 1)
-            if TOKEN_TILES <= tick - PASSES + 1 < PIECES:
-                tile_passes(*piece_of(tick - PASSES + 1))
-            if tick >= UNITS - PASSES and tick < UNITS - 1:
-                late_passes(tick - UNITS + PASSES)
-            if tick + 2 < UNITS:
-                pass_through(tick + 2)
-            if tick == UNITS - 2:
-                late_passes(PASSES - 1)
+        for u in range(PASSES):
+            interleave(u)
+            if u == 0:
+                interleave_s(0)
+            else:
+                x_transposes(u)
+                if u + 1 < PASSES:
+                    pass_through(u + 1)
+                if u == 1:
+                    build_tables()
+                quantize_x(u - 1)
+            quantize_w(u)
+            if u + 2 < PASSES:
+                widen_s(u + 2)
+                widen_v(u + 2)
+            if u + 1 < PASSES:
+                x_copies(u, nc.scalar.copy)
+                interleave_s(u + 1)
+        last = PASSES - 1
+        for m in range(2):
+            multiply(0, m, range(last))
+        widen_s(PASSES)
+        for m in range(2):
+            multiply(0, m, (last,))
+        multiply(0, 2, range(PASSES))
+        pass_through(PASSES)
+        x_copies(TOKEN_TILES - 1, nc.vector.tensor_copy)
+        interleave(PASSES)
+        rope_products(0)
+        quantize_x(TOKEN_TILES - 1)
+        multiply(0, TOKEN_TILES - 1, range(PASSES))
+        widen_s(PASSES + 1)
+        interleave_s(PASSES)
+        pass_through(PASSES + 1)
+
+        waiting = [0]
+        for u in range(PASSES, UNITS - 2):
+            piece = u - PASSES + (1 if u < 2 * PASSES else 0)
+            rotates = u != 2 * PASSES - 1
+            widen_s(u + 2)
+            interleave_s(u + 1)
+            if len(waiting) == 2 or not rotates:
+                rope_sum(waiting.pop(0), nc.vector)
+            interleave(u + 1)
+            quantize_w(u)
+            if u >= 2 * PASSES - 1:
+                c, m = piece_of(u - PASSES + 1)
+                multiply(c, m, range(PASSES))
+            if u >= UNITS - PASSES:
                 for m in range(TOKEN_TILES):
-                    plain_copy(CHUNKS - 1, m, True)
-            if products:
-                rope_products(*piece_of(piece))
-                pending.append(piece)
-        for piece in pending:
-            rope_sum(*piece_of(piece))
+                    multiply(CHUNKS - 1, m, (u % PASSES,))
+            pass_through(u + 2)
+            if rotates:
+                rope_products(piece)
+                waiting.append(piece)
+
+        u = UNITS - 2
+        interleave_s(u + 1)
+        rope_sum(PIECES - 4, nc.vector)
+        interleave(u + 1)
+        quantize_w(u)
+        quantize_w(u + 1)
+        multiply(ROPE_CHUNKS - 1, TOKEN_TILES - 1, range(PASSES))
+        for m in range(TOKEN_TILES):
+            multiply(CHUNKS - 1, m, (PASSES - 2, PASSES - 1))
+            value_copy(m)
+        rope_sum(PIECES - 3, nc.vector)
+        rope_products(PIECES - 2)
+        rope_products(PIECES - 1)
+        rope_sum(PIECES - 2, nc.vector)
+        rope_sum(PIECES - 1, nc.vector)

@@ -27,10 +27,10 @@ UNITS = CHUNKS * PASSES
 PIECES = ROPE_CHUNKS * TOKEN_TILES
 HEAD = 128
 
-TENSOR_COLS = 176
-GPSIMD_COLS = 184
+TENSOR_COLS = 128
+GPSIMD_COLS = 192
 RUN = 4
-VECTOR_PLANES = (2, 1, 1, 1)
+VECTOR_PLANES = (2, 2, 1, 1)
 
 
 def tile_quantllamaattentionfused_pa_kernel(tc, x, w_qkv_bytes, w_qkv_scale, cos, sin, out_0, out_1, out_2):
@@ -148,7 +148,7 @@ def tile_quantllamaattentionfused_pa_kernel(tc, x, w_qkv_bytes, w_qkv_scale, cos
 
         def pass_through(u):
             pil = psum_il.tile([P, CHUNK * 2], BF16, name="pil", tag="pil")
-            for n0, n1 in ((0, 128), (128, TENSOR_COLS)):
+            for n0, n1 in ((0, TENSOR_COLS),):
                 nc.tensor.matmul(
                     out=pil[:, n0 * PACK : n1 * PACK].rearrange("p (n t) -> p n t", t=PACK),
                     lhsT=ident_bf[:],

@@ -331,10 +331,10 @@ def tile_quantllamaattentionfused_pa_kernel(tc, x, w_qkv_bytes, w_qkv_scale, cos
             if u >= 2 * PASSES - 1:
                 c, m = piece_of(u - PASSES + 1)
                 multiply(c, m, range(PASSES))
+            pass_through(u + 2)
             if u >= UNITS - PASSES:
                 for m in range(TOKEN_TILES):
                     multiply(CHUNKS - 1, m, (u % PASSES,))
-            pass_through(u + 2)
             if rotates:
                 rope_products(piece)
                 waiting.append(piece)
@@ -349,8 +349,8 @@ def tile_quantllamaattentionfused_pa_kernel(tc, x, w_qkv_bytes, w_qkv_scale, cos
         for m in range(TOKEN_TILES):
             multiply(CHUNKS - 1, m, (PASSES - 2, PASSES - 1))
             value_copy(m)
-        rope_sum(PIECES - 3, nc.vector)
+        rope_sum(PIECES - 3, nc.gpsimd)
         rope_products(PIECES - 2)
         rope_products(PIECES - 1)
-        rope_sum(PIECES - 2, nc.vector)
+        rope_sum(PIECES - 2, nc.gpsimd)
         rope_sum(PIECES - 1, nc.vector)

from contextlib import ExitStack

import concourse.mybir as mybir
from concourse.masks import make_identity

F32 = mybir.dt.float32
BF16 = mybir.dt.bfloat16
U32 = mybir.dt.uint32
U8 = mybir.dt.uint8
FP8 = mybir.dt.float8_e4m3fn
FP8X4 = mybir.dt.float8_e4m3fn_x4
MULT = mybir.AluOpType.mult
ADD = mybir.AluOpType.add
COPY = mybir.ActivationFunctionType.Copy

TOKENS, HIDDEN, FEATURES = 512, 2048, 3072
FLOPS = 2 * TOKENS * HIDDEN * FEATURES

P = 128
PACK = 4
PASSES = HIDDEN // (P * PACK)
TOKEN_TILES = TOKENS // P
CHUNK = 512
CHUNKS = FEATURES // CHUNK
ROPE_CHUNKS = 5
UNITS = CHUNKS * PASSES
PIECES = ROPE_CHUNKS * TOKEN_TILES
HEAD = 128

TENSOR_COLS = 128
GPSIMD_COLS = 192
RUN = 4
VECTOR_PLANES = (2, 2, 1, 1)


def tile_quantllamaattentionfused_pa_kernel(tc, x, w_qkv_bytes, w_qkv_scale, cos, sin, out_0, out_1, out_2):
    nc = tc.nc
    x_rows = x.rearrange("b s h -> (b s) h")
    w_view = w_qkv_bytes.rearrange("(g p t) n -> g p t n", p=P, t=PACK)
    q_rows = out_0.rearrange("b s h d -> (b s) (h d)")
    k_rows = out_1.rearrange("b s h d -> (b s) (h d)")
    v_rows = out_2.rearrange("b s h d -> (b s) (h d)")

    def out_block(c, m):
        rows = slice(m * P, (m + 1) * P)
        if c < ROPE_CHUNKS - 1:
            return q_rows[rows, c * CHUNK : (c + 1) * CHUNK]
        return (k_rows if c < ROPE_CHUNKS else v_rows)[rows, :]

    def piece_of(piece):
        return divmod(piece, TOKEN_TILES)

    with ExitStack() as ctx:
        const = ctx.enter_context(tc.tile_pool(name="const", bufs=1))
        xin_pool = ctx.enter_context(tc.tile_pool(name="xin", bufs=TOKEN_TILES))
        xq_pool = ctx.enter_context(tc.tile_pool(name="xq", bufs=TOKEN_TILES))
        wb_pool = ctx.enter_context(tc.tile_pool(name="wbytes", bufs=2 * PASSES))
        wide_pool = ctx.enter_context(tc.tile_pool(name="wide", bufs=6))
        head_pool = ctx.enter_context(tc.tile_pool(name="head", bufs=PASSES))
        grp_pool = ctx.enter_context(tc.tile_pool(name="grp", bufs=3))
        code_pool = ctx.enter_context(tc.tile_pool(name="codes", bufs=10))
        rope_pool = ctx.enter_context(tc.tile_pool(name="rope", bufs=5))
        res_pool = ctx.enter_context(tc.tile_pool(name="res", bufs=4))
        val_pool = ctx.enter_context(tc.tile_pool(name="val", bufs=TOKEN_TILES))
        psum = ctx.enter_context(tc.psum_pool(name="psum", bufs=6))
        psum_il = ctx.enter_context(tc.psum_pool(name="psum_il", bufs=2))
        ctx.enter_context(tc.manual_schedule())

        ident = const.tile([P, P], F32, name="ident")
        make_identity(nc, ident[:])
        ident_bf = const.tile([P, P], BF16, name="ident_bf")
        make_identity(nc, ident_bf[:])

        w_scale = const.tile([P, PASSES, PACK], F32, name="w_scale")
        nc.scalar.dma_start(out=w_scale[:], in_=w_qkv_scale.rearrange("(g p t) o -> p g (t o)", p=P, t=PACK))
        cos_in = const.tile([P, TOKEN_TILES, HEAD // 2], BF16, name="cos_in")
        nc.scalar.dma_start(out=cos_in[:], in_=cos.rearrange("(m p) j -> p m j", p=P))
        sin_in = const.tile([P, TOKEN_TILES, HEAD // 2], BF16, name="sin_in")
        nc.scalar.dma_start(out=sin_in[:], in_=sin.rearrange("(m p) j -> p m j", p=P))

        warm = const.tile([P, 2], F32, name="warm")
        nc.vector.memset(warm[:], 0.0)
        nc.scalar.activation(out=warm[:, 1:2], in_=warm[:, 0:1], func=COPY)

        w_bytes = {}
        x_in = []
        for c, width in ((0, 1), (1, 2), (3, 2), (5, 1)):
            for g in range(PASSES):
                wb = wb_pool.tile([P, PACK, width * CHUNK], U8, name="wb", tag="wb%d" % width)
                for i in range(width):
                    w_bytes[(c + i) * PASSES + g] = wb[:, :, i * CHUNK : (i + 1) * CHUNK]
                source = w_view[g][:, :, c * CHUNK : (c + width) * CHUNK]
                if c == 0 and g == 0:
                    for t in range(PACK):
                        nc.sync.dma_start(out=wb[:, t, :], in_=source[:, t, :])
                else:
                    nc.sync.dma_start(out=wb[:], in_=source)
                if (c == 0 and g > 0) or (c == 1 and g == 0):
                    m = len(x_in)
                    xi = xin_pool.tile([P, HIDDEN], BF16, name="xi", tag="xi")
                    nc.sync.dma_start(out=xi[:], in_=x_rows[m * P : (m + 1) * P, :])
                    x_in.append(xi)

        tables = const.tile([P, TOKEN_TILES, 2, HEAD], F32, name="tables")

        wide = {}
        passed = {}
        grouped = {}
        w_codes = {}
        x_banks = {}
        x_grouped = {}
        x_codes = {}
        acc = {}
        prod = {}

        def build_tables():
            cos2 = tables[:, :, 0, :].rearrange("p m (j e) -> p m j e", e=2)
            sin2 = tables[:, :, 1, :].rearrange("p m (j e) -> p m j e", e=2)
            cos_pairs = cos_in[:].unsqueeze(3).to_broadcast([P, TOKEN_TILES, HEAD // 2, 2])
            nc.vector.tensor_copy(out=cos2, in_=cos_pairs)
            nc.vector.tensor_copy(out=sin2[:, :, :, 0], in_=sin_in[:])
            nc.vector.tensor_scalar(out=sin2[:, :, :, 1], in0=sin_in[:], scalar1=-1.0, scalar2=None, op0=MULT)

        def wide_tile(u):
            if u not in wide:
                wd = wide_pool.tile([P, PACK, CHUNK], BF16, name="wd", tag="wd")
                wide[u] = wd
            return wide[u]

        def widen_v(u):
            for t in range(PACK - VECTOR_PLANES[u], PACK):
                nc.vector.tensor_scalar(
                    out=wide_tile(u)[:, t, :],
                    in0=w_bytes[u][:, t, :].bitcast(FP8),
                    scalar1=w_scale[:, u % PASSES, t : t + 1],
                    scalar2=None,
                    op0=MULT,
                )

        def widen_s(u):
            for t in range(PACK - (VECTOR_PLANES[u] if u < PASSES else 0)):
                nc.scalar.activation(
                    out=wide_tile(u)[:, t, :],
                    in_=w_bytes[u][:, t, :].bitcast(FP8),
                    func=COPY,
                    scale=w_scale[:, u % PASSES, t : t + 1],
                )

        def pass_through(u):
            pil = psum_il.tile([P, CHUNK * 2], BF16, name="pil", tag="pil")
            for n0, n1 in ((0, TENSOR_COLS),):
                nc.tensor.matmul(
                    out=pil[:, n0 * PACK : n1 * PACK].rearrange("p (n t) -> p n t", t=PACK),
                    lhsT=ident_bf[:],
                    rhs=wide[u][:, :, n0:n1].rearrange("p t n -> p n t"),
                    start=True,
                    stop=True,
                )
            passed[u] = pil

        def group(u):
            if u not in grouped:
                if u < PASSES:
                    gr = head_pool.tile([P, CHUNK, PACK], BF16, name="gh", tag="gh", align_bytes=64)
                else:
                    gr = grp_pool.tile([P, CHUNK, PACK], BF16, name="gr", tag="gr", align_bytes=64)
                grouped[u] = gr
            return grouped[u]

        def gpsimd_cols(u):
            return GPSIMD_COLS if PASSES <= u < UNITS - 1 else 0

        def interleave_s(u):
            nc.scalar.copy(
                out=group(u)[:, :TENSOR_COLS, :].rearrange("p n t -> p (n t)").bitcast(F32),
                in_=passed[u][:, : TENSOR_COLS * PACK].bitcast(F32),
            )

        def interleave(u):
            gr = group(u)
            cut = CHUNK - gpsimd_cols(u)
            end = min(cut + RUN, CHUNK)
            nc.vector.tensor_copy(
                out=gr[:, TENSOR_COLS:end, :].rearrange("p (c i) t -> p c t i", i=RUN),
                in_=wide[u][:, :, TENSOR_COLS:end].rearrange("p t (c i) -> p c t i", i=RUN),
            )
            if cut < CHUNK:
                nc.gpsimd.tensor_scalar(
                    out=gr[:, cut:, :],
                    in0=wide[u][:, :, cut:].rearrange("p t n -> p n t"),
                    scalar1=1.0,
                    scalar2=0.0,
                    op0=MULT,
                    op1=ADD,
                )

        def quantize_w(u):
            wc = code_pool.tile([P, CHUNK], U32, name="wc", tag="wc", align_bytes=64)
            ws = code_pool.tile([P, CHUNK], U8, name="ws", tag="ws", align_bytes=64)
            nc.vector.quantize_mx(
                out=wc[:].bitcast(FP8X4), scales=ws[:], in_=grouped[u][:].rearrange("p n t -> p (n t)")
            )
            w_codes[u] = (wc, ws)

        def x_transposes(m):
            words = x_in[m][:].bitcast(F32)
            banks = []
            for half in range(2):
                xt = psum.tile([P, CHUNK], F32, name="acc", tag="acc")
                for q in range(4):
                    g = 2 * half + q // 2
                    first = 256 * g + q % 2
                    nc.tensor.transpose(xt[:, q * P : (q + 1) * P], words[:, first : 256 * (g + 1) : 2], ident[:])
                banks.append(xt)
            x_banks[m] = banks

        def x_copies(m, copy):
            xg = xq_pool.tile([P, PASSES * P * PACK], BF16, name="xg", tag="xg", align_bytes=64)
            xg_words = xg[:].bitcast(F32).rearrange("p (g r u) -> p g r u", g=PASSES, u=2)
            for half in range(2):
                copy(
                    out=xg_words[:, 2 * half : 2 * half + 2],
                    in_=x_banks[m][half][:].rearrange("p (g u r) -> p g r u", g=2, u=2),
                )
            x_grouped[m] = xg

        def quantize_x(m):
            xc = xq_pool.tile([P, PASSES * P], U32, name="xc", tag="xc", align_bytes=64)
            xs = xq_pool.tile([P, PASSES * P], U8, name="xs", tag="xs", align_bytes=64)
            nc.vector.quantize_mx(out=xc[:].bitcast(FP8X4), scales=xs[:], in_=x_grouped[m][:])
            x_codes[m] = (xc, xs)

        def multiply(c, m, passes):
            for g in passes:
                if g == 0:
                    bank = psum.tile([P, CHUNK], F32, name="acc", tag="acc")
                    acc[(c, m)] = bank
                xc, xs = x_codes[m]
                wc, ws = w_codes[c * PASSES + g]
                cols = slice(g * P, (g + 1) * P)
                nc.tensor.matmul_mx(
                    out=acc[(c, m)][:],
                    lhsT=xc[:, cols].bitcast(FP8X4),
                    lhsT_scale=xs[:, cols],
                    rhs=wc[:].bitcast(FP8X4),
                    rhs_scale=ws[:],
                    start=(g == 0),
                    stop=(g == PASSES - 1),
                )

        def rope_products(piece):
            c, m = piece_of(piece)
            pab = rope_pool.tile([P, 2, CHUNK], F32, name="pab", tag="pab")
            shape = [P, 2, CHUNK // HEAD, HEAD]
            nc.vector.tensor_tensor(
                out=pab[:].rearrange("p s (h f) -> p s h f", f=HEAD),
                in0=acc[(c, m)][:].rearrange("p (h f) -> p h f", f=HEAD).unsqueeze(1).to_broadcast(shape),
                in1=tables[:, m, :, :].unsqueeze(2).to_broadcast(shape),
                op=MULT,
            )
            prod[piece] = pab

        def rope_sum(piece, engine):
            pab = prod[piece]
            res = res_pool.tile([P, CHUNK], F32, name="res", tag="res")
            engine.tensor_tensor(
                out=res[:].rearrange("p (j e) -> p j e", e=2),
                in0=pab[:, 0, :].rearrange("p (j e) -> p j e", e=2),
                in1=pab[:, 1, :].rearrange("p (j e) -> p j e", e=2)[:, :, ::-1],
                op=ADD,
            )
            nc.sync.dma_start(out=out_block(*piece_of(piece)), in_=res[:])

        def value_copy(m):
            val = val_pool.tile([P, CHUNK], F32, name="val", tag="val")
            nc.scalar.copy(out=val[:], in_=acc[(CHUNKS - 1, m)][:])
            nc.scalar.dma_start(out=out_block(CHUNKS - 1, m), in_=val[:])

        widen_v(0)
        widen_s(0)
        widen_s(1)
        widen_v(1)
        pass_through(0)
        x_transposes(0)
        pass_through(1)
        for u in range(PASSES):
            interleave(u)
            if u == 0:
                interleave_s(0)
            else:
                x_transposes(u)
                if u + 1 < PASSES:
                    pass_through(u + 1)
                if u == 1:
                    build_tables()
                quantize_x(u - 1)
            quantize_w(u)
            if u + 2 < PASSES:
                widen_s(u + 2)
                widen_v(u + 2)
            if u + 1 < PASSES:
                x_copies(u, nc.scalar.copy)
                interleave_s(u + 1)
        last = PASSES - 1
        for m in range(2):
            multiply(0, m, range(last))
        widen_s(PASSES)
        for m in range(2):
            multiply(0, m, (last,))
        multiply(0, 2, range(PASSES))
        pass_through(PASSES)
        x_copies(TOKEN_TILES - 1, nc.vector.tensor_copy)
        interleave(PASSES)
        rope_products(0)
        quantize_x(TOKEN_TILES - 1)
        multiply(0, TOKEN_TILES - 1, range(PASSES))
        widen_s(PASSES + 1)
        interleave_s(PASSES)
        pass_through(PASSES + 1)

        waiting = [0]
        for u in range(PASSES, UNITS - 2):
            piece = u - PASSES + (1 if u < 2 * PASSES else 0)
            rotates = u != 2 * PASSES - 1
            widen_s(u + 2)
            interleave_s(u + 1)
            if len(waiting) == 2 or not rotates:
                rope_sum(waiting.pop(0), nc.vector)
            interleave(u + 1)
            quantize_w(u)
            if u >= 2 * PASSES - 1:
                c, m = piece_of(u - PASSES + 1)
                multiply(c, m, range(PASSES))
            pass_through(u + 2)
            if u >= UNITS - PASSES:
                for m in range(TOKEN_TILES):
                    multiply(CHUNKS - 1, m, (u % PASSES,))
            if rotates:
                rope_products(piece)
                waiting.append(piece)

        u = UNITS - 2
        interleave_s(u + 1)
        rope_sum(PIECES - 4, nc.vector)
        interleave(u + 1)
        quantize_w(u)
        quantize_w(u + 1)
        multiply(ROPE_CHUNKS - 1, TOKEN_TILES - 1, range(PASSES))
        for m in range(TOKEN_TILES):
            multiply(CHUNKS - 1, m, (PASSES - 2, PASSES - 1))
            value_copy(m)
        rope_sum(PIECES - 3, nc.gpsimd)
        rope_products(PIECES - 2)
        rope_products(PIECES - 1)
        rope_sum(PIECES - 2, nc.gpsimd)
        rope_sum(PIECES - 1, nc.vector)
